import numpy as np
import ml_dtypes


def mxq(x, axis, fmt="e4m3"):
    dtype, down = {"e4m3": (ml_dtypes.float8_e4m3fn, 7), "e5m2": (ml_dtypes.float8_e5m2, 14)}[fmt]
    v = np.moveaxis(np.asarray(x, np.float32).astype(ml_dtypes.bfloat16).astype(np.float64), axis, -1)
    blocks = v.reshape(v.shape[:-1] + (-1, 32))
    amax = np.abs(blocks).max(-1, keepdims=True)
    byte = np.maximum(np.where(amax > 0, np.frexp(amax)[1] - 1 + 127, 0) - down, 1)
    scale = np.exp2(byte - 127.0)
    codes = (blocks / scale).astype(np.float32).astype(dtype).astype(np.float64)
    return np.moveaxis((codes * scale).reshape(v.shape), -1, axis)


WIDE = False


def mx_kscale(k):
    if not WIDE:
        return np.ones(k)
    levels = np.array([10, -10, 5, -5, 0])
    a = np.random.permutation(np.resize(levels, k // 512 * 4)).reshape(k // 512, 4)
    idx = np.arange(k)
    return np.exp2(a[idx // 512, idx % 128 // 32])


BF16 = ml_dtypes.bfloat16


def bf(x):
    return np.asarray(x, np.float32).astype(BF16)


def f64(x):
    return np.asarray(x).astype(np.float64)


M, N, D = 128, 16384, 512
TINY = 1e-12


def l2norm(x):
    n = np.sqrt((x * x).sum(1, keepdims=True))
    return x / np.maximum(n, TINY)


def setup_inputs():
    s = mx_kscale(N)
    a = np.random.standard_normal((M, N)) * 1.2
    e = np.exp(a - a.max(1, keepdims=True))
    xi = e / e.sum(1, keepdims=True)
    return {"xi": bf(xi * s), "memory": bf(np.random.standard_normal((N, D)) * 0.35 / s[:, None])}


def reference(xi, memory):
    mem = f64(memory)
    output = mxq(f64(xi), 1, "e4m3") @ mxq(mem, 0, "e4m3")
    mem_n = l2norm(mem)
    return mxq(l2norm(output), 1, "e4m3") @ mxq(mem_n, 1, "e4m3").T

@@ -1,0 +1,232 @@
+from contextlib import ExitStack
+
+import concourse.mybir as mybir
+from concourse.masks import make_identity
+
+F32 = mybir.dt.float32
+BF16 = mybir.dt.bfloat16
+U32 = mybir.dt.uint32
+U8 = mybir.dt.uint8
+FP8X4 = mybir.dt.float8_e4m3fn_x4
+ACT = mybir.ActivationFunctionType
+
+P = 128
+PACK = 4
+K_PASS = P * PACK
+PAIR = 2
+
+QUERIES = 128
+PATTERNS = 16384
+FEATURES = 512
+TINY = 1e-12
+
+PASSES = 4
+CHUNK = PASSES * K_PASS
+CHUNKS = PATTERNS // CHUNK
+LAG = 4
+
+FLOPS = 2 * 2 * QUERIES * PATTERNS * FEATURES
+
+assert QUERIES == P and FEATURES == K_PASS and CHUNKS * CHUNK == PATTERNS
+
+
+def tile_hopfieldretrievalmodel_pa_k_kernel(tc, xi, memory, out):
+    nc = tc.nc
+    with ExitStack() as stack:
+        consts = stack.enter_context(tc.tile_pool(name="consts", bufs=1))
+        rows_pool = stack.enter_context(tc.tile_pool(name="rows", bufs=min(CHUNKS, LAG + 2)))
+        unit_pool = stack.enter_context(tc.tile_pool(name="unit", bufs=CHUNKS - LAG + 1))
+        norm_pool = stack.enter_context(tc.tile_pool(name="norm", bufs=min(CHUNKS, LAG + 2)))
+        xi_pool = stack.enter_context(tc.tile_pool(name="xi", bufs=2))
+        stage = stack.enter_context(tc.tile_pool(name="stage", bufs=3))
+        turned_pool = stack.enter_context(tc.psum_pool(name="turned", bufs=4))
+        output_pool = stack.enter_context(tc.psum_pool(name="output", bufs=1))
+        pair_pool = stack.enter_context(tc.psum_pool(name="pair", bufs=3))
+
+        identity = consts.tile([P, P], F32)
+        make_identity(nc, identity[:])
+
+        one = consts.tile([P, 1], F32)
+        nc.vector.memset(one[:], 1.0)
+        warm = consts.tile([P, 1], F32)
+        nc.scalar.sqrt(warm[:], one[:])
+
+        output = output_pool.tile([QUERIES, FEATURES], F32)
+
+        xi_of = {}
+        rows_of = {}
+        inverse_norm_of = {}
+        unit_codes_of = {}
+        unit_scales_of = {}
+
+        def inverse_norm(result, sum_of_squares):
+            nc.vector.tensor_scalar_max(sum_of_squares, sum_of_squares, TINY * TINY)
+            nc.scalar.sqrt(sum_of_squares, sum_of_squares)
+            nc.vector.reciprocal(result, sum_of_squares)
+
+        def load(chunk):
+            first = chunk * CHUNK
+            xi_of[chunk] = xi_pool.tile([QUERIES, CHUNK], BF16, name="xi_columns")
+            nc.sync.dma_start(out=xi_of[chunk][:], in_=xi[:, first : first + CHUNK])
+            rows_of[chunk] = rows_pool.tile([P, PASSES, PACK, FEATURES], BF16, name="rows")
+            source = memory[first : first + CHUNK, :].rearrange(
+                "(g p t) d -> g p t d", g=PASSES, t=PACK
+            )
+            for g in range(PASSES):
+                nc.sync.dma_start(out=rows_of[chunk][:, g], in_=source[g])
+
+        def retrieve(chunk):
+            xi_words = xi_of[chunk][:].bitcast(F32).rearrange(
+                "q (g p u) -> q g u p", g=PASSES, u=PAIR
+            )
+            xi_grouped = xi_pool.tile([P, PASSES * QUERIES * PACK], BF16, align_bytes=64)
+            xi_grouped_words = xi_grouped[:].bitcast(F32).rearrange(
+                "p (g q u) -> p g q u", g=PASSES, u=PAIR
+            )
+            for half in range(PASSES // 2):
+                xi_turned = turned_pool.tile([P, 2, PAIR, QUERIES], F32, tag="turned")
+                for g in range(2):
+                    for u in range(PAIR):
+                        nc.tensor.transpose(
+                            xi_turned[:, g, u, :], xi_words[:, 2 * half + g, u, :], identity[:]
+                        )
+                nc.vector.tensor_copy(
+                    out=xi_grouped_words[:, 2 * half : 2 * half + 2],
+                    in_=xi_turned[:].rearrange("p g u q -> p g q u"),
+                )
+            xi_codes = xi_pool.tile([P, PASSES * QUERIES], U32, align_bytes=64)
+            xi_scales = xi_pool.tile([P, PASSES * QUERIES], U8, align_bytes=64)
+            nc.vector.quantize_mx(
+                out=xi_codes[:].bitcast(FP8X4), scales=xi_scales[:], in_=xi_grouped[:]
+            )
+
+            for g in range(PASSES):
+                grouped = stage.tile([P, FEATURES, PACK], BF16, align_bytes=64)
+                nc.vector.tensor_copy(
+                    out=grouped[:].rearrange("p (c i) t -> p c t i", i=4),
+                    in_=rows_of[chunk][:, g].rearrange("p t (c i) -> p c t i", i=4),
+                )
+                codes = stage.tile([P, FEATURES], U32, align_bytes=64)
+                scales = stage.tile([P, FEATURES], U8, align_bytes=64)
+                nc.vector.quantize_mx(
+                    out=codes[:].bitcast(FP8X4),
+                    scales=scales[:],
+                    in_=grouped[:].rearrange("p d t -> p (d t)"),
+                )
+                queries = slice(g * QUERIES, (g + 1) * QUERIES)
+                nc.tensor.matmul_mx(
+                    out=output[:],
+                    lhsT=xi_codes[:, queries].bitcast(FP8X4),
+                    lhsT_scale=xi_scales[:, queries],
+                    rhs=codes[:].bitcast(FP8X4),
+                    rhs_scale=scales[:],
+                    start=(chunk == 0 and g == 0),
+                    stop=(chunk == CHUNKS - 1 and g == PASSES - 1),
+                )
+
+            sum_of_squares = norm_pool.tile([P, PASSES * PACK], F32)
+            for g in range(PASSES):
+                for t in range(PACK):
+                    squares = stage.tile([P, FEATURES], BF16)
+                    nc.scalar.activation(
+                        out=squares[:],
+                        in_=rows_of[chunk][:, g, t, :],
+                        func=ACT.Square,
+                        accum_out=sum_of_squares[:, g * PACK + t : g * PACK + t + 1],
+                    )
+            inverse_norm_of[chunk] = norm_pool.tile([P, PASSES * PACK], F32, name="inverse_norm")
+            inverse_norm(inverse_norm_of[chunk][:], sum_of_squares[:])
+
+        def turn_and_group(grouped_words, row_words, copy):
+            turned = turned_pool.tile([P, 2, PAIR, P], F32, tag="turned")
+            for i in range(2):
+                for u in range(PAIR):
+                    nc.tensor.transpose(
+                        turned[:, i, u, :], row_words[:, i, u * P : (u + 1) * P], identity[:]
+                    )
+            copy(out=grouped_words, in_=turned[:].rearrange("c i u r -> c i r u"))
+
+        def prepare(chunk):
+            unit_codes_of[chunk] = unit_pool.tile([P, CHUNK], U32, name="unit_codes", align_bytes=64)
+            unit_scales_of[chunk] = unit_pool.tile([P, CHUNK], U8, name="unit_scales", align_bytes=64)
+            for g in range(PASSES):
+                unit = stage.tile([P, PACK, FEATURES], BF16)
+                for t in range(PACK):
+                    nc.vector.tensor_scalar_mul(
+                        out=unit[:, t, :],
+                        in0=rows_of[chunk][:, g, t, :],
+                        scalar1=inverse_norm_of[chunk][:, g * PACK + t : g * PACK + t + 1],
+                    )
+                unit_grouped = stage.tile([P, K_PASS * PACK], BF16, align_bytes=64)
+                unit_grouped_words = unit_grouped[:].bitcast(F32).rearrange(
+                    "c (t p u) -> c t p u", t=PACK, u=PAIR
+                )
+                unit_words = unit[:].bitcast(F32)
+                for half in range(PACK // 2):
+                    both = slice(2 * half, 2 * half + 2)
+                    turn_and_group(unit_grouped_words[:, both], unit_words[:, both], nc.scalar.copy)
+                columns = slice(g * K_PASS, (g + 1) * K_PASS)
+                nc.vector.quantize_mx(
+                    out=unit_codes_of[chunk][:, columns].bitcast(FP8X4),
+                    scales=unit_scales_of[chunk][:, columns],
+                    in_=unit_grouped[:],
+                )
+
+        def normalise_output():
+            squares = stage.tile([QUERIES, FEATURES], BF16)
+            sum_of_squares = consts.tile([QUERIES, 1], F32, name="output_sum_of_squares")
+            nc.scalar.activation(
+                out=squares[:], in_=output[:], func=ACT.Square, accum_out=sum_of_squares[:]
+            )
+            inverse = consts.tile([QUERIES, 1], F32, name="output_inverse_norm")
+            inverse_norm(inverse[:], sum_of_squares[:])
+            unit = consts.tile([QUERIES, FEATURES], BF16, name="unit_output")
+            nc.vector.tensor_scalar_mul(out=unit[:], in0=output[:], scalar1=inverse[:])
+            unit_words = unit[:].bitcast(F32)
+            turned = turned_pool.tile([P, PAIR, QUERIES], F32, tag="turned")
+            for u in range(PAIR):
+                nc.tensor.transpose(turned[:, u, :], unit_words[:, u * P : (u + 1) * P], identity[:])
+            grouped = consts.tile([P, QUERIES * PACK], BF16, name="unit_output_grouped", align_bytes=64)
+            nc.vector.tensor_copy(
+                out=grouped[:].bitcast(F32).rearrange("c (q u) -> c q u", u=PAIR),
+                in_=turned[:].rearrange("c u q -> c q u"),
+            )
+            codes = consts.tile([P, QUERIES], U32, name="unit_output_codes", align_bytes=64)
+            scales = consts.tile([P, QUERIES], U8, name="unit_output_scales", align_bytes=64)
+            nc.vector.quantize_mx(out=codes[:].bitcast(FP8X4), scales=scales[:], in_=grouped[:])
+            return codes, scales
+
+        def cosines(chunk, output_codes, output_scales):
+            for g in range(PASSES):
+                columns = slice(g * K_PASS, (g + 1) * K_PASS)
+                pair = pair_pool.tile([QUERIES, K_PASS], F32)
+                nc.tensor.matmul_mx(
+                    out=pair[:],
+                    lhsT=output_codes[:].bitcast(FP8X4),
+                    lhsT_scale=output_scales[:],
+                    rhs=unit_codes_of[chunk][:, columns].bitcast(FP8X4),
+                    rhs_scale=unit_scales_of[chunk][:, columns],
+                    start=True,
+                    stop=True,
+                )
+                ordered = stage.tile([QUERIES, K_PASS], F32)
+                copy = nc.vector.tensor_copy if g % 2 == 0 else nc.scalar.copy
+                copy(
+                    out=ordered[:].rearrange("q (p t) -> q p t", t=PACK),
+                    in_=pair[:].rearrange("q (t p) -> q p t", t=PACK),
+                )
+                first = chunk * CHUNK + g * K_PASS
+                nc.sync.dma_start(out=out[:, first : first + K_PASS], in_=ordered[:])
+
+        load(0)
+        for chunk in range(CHUNKS):
+            if chunk + 1 < CHUNKS:
+                load(chunk + 1)
+            retrieve(chunk)
+            if chunk >= LAG:
+                prepare(chunk - LAG)
+        output_codes, output_scales = normalise_output()
+        for chunk in range(CHUNKS):
+            if chunk >= CHUNKS - LAG:
+                prepare(chunk)
+            cosines(chunk, output_codes, output_scales)

@@ -67,12 +67,13 @@ def tile_hopfieldretrievalmodel_pa_k_kernel(tc, xi, memory, out):
         def load(chunk):
             first = chunk * CHUNK
             xi_of[chunk] = xi_pool.tile([QUERIES, CHUNK], BF16, name="xi_columns")
-            nc.sync.dma_start(out=xi_of[chunk][:], in_=xi[:, first : first + CHUNK])
             rows_of[chunk] = rows_pool.tile([P, PASSES, PACK, FEATURES], BF16, name="rows")
             source = memory[first : first + CHUNK, :].rearrange(
                 "(g p t) d -> g p t d", g=PASSES, t=PACK
             )
-            for g in range(PASSES):
+            nc.sync.dma_start(out=rows_of[chunk][:, 0], in_=source[0])
+            nc.sync.dma_start(out=xi_of[chunk][:], in_=xi[:, first : first + CHUNK])
+            for g in range(1, PASSES):
                 nc.sync.dma_start(out=rows_of[chunk][:, g], in_=source[g])
 
         def retrieve(chunk):
@@ -210,7 +211,7 @@ def tile_hopfieldretrievalmodel_pa_k_kernel(tc, xi, memory, out):
                     stop=True,
                 )
                 ordered = stage.tile([QUERIES, K_PASS], F32)
-                copy = nc.vector.tensor_copy if g % 2 == 0 else nc.scalar.copy
+                copy = nc.scalar.copy if g == PASSES - 1 else nc.vector.tensor_copy
                 copy(
                     out=ordered[:].rearrange("q (p t) -> q p t", t=PACK),
                     in_=pair[:].rearrange("q (t p) -> q p t", t=PACK),

@@ -20,32 +20,66 @@ PATTERNS = 16384
 FEATURES = 512
 TINY = 1e-12
 
-PASSES = 4
-CHUNK = PASSES * K_PASS
-CHUNKS = PATTERNS // CHUNK
-LAG = 4
+PASSES = PATTERNS // K_PASS
+GROUP = 4
+GROUPS = PASSES // GROUP
+LAG = 14
+AHEAD = 4
 
 FLOPS = 2 * 2 * QUERIES * PATTERNS * FEATURES
 
-assert QUERIES == P and FEATURES == K_PASS and CHUNKS * CHUNK == PATTERNS
+assert QUERIES == P and FEATURES == K_PASS and GROUPS * GROUP == PASSES
 
 
 def tile_hopfieldretrievalmodel_pa_k_kernel(tc, xi, memory, out):
     nc = tc.nc
     with ExitStack() as stack:
         consts = stack.enter_context(tc.tile_pool(name="consts", bufs=1))
-        rows_pool = stack.enter_context(tc.tile_pool(name="rows", bufs=min(CHUNKS, LAG + 2)))
-        unit_pool = stack.enter_context(tc.tile_pool(name="unit", bufs=CHUNKS - LAG + 1))
-        norm_pool = stack.enter_context(tc.tile_pool(name="norm", bufs=min(CHUNKS, LAG + 2)))
-        xi_pool = stack.enter_context(tc.tile_pool(name="xi", bufs=2))
+        rows_pool = stack.enter_context(tc.tile_pool(name="rows", bufs=LAG + AHEAD + 2))
+        unit_pool = stack.enter_context(tc.tile_pool(name="unit", bufs=PASSES - LAG + 3))
+        norm_pool = stack.enter_context(tc.tile_pool(name="norm", bufs=LAG // GROUP + 3))
+        xi_pool = stack.enter_context(tc.tile_pool(name="xi", bufs=3))
         stage = stack.enter_context(tc.tile_pool(name="stage", bufs=3))
+        store_pool = stack.enter_context(tc.tile_pool(name="store", bufs=6))
         turned_pool = stack.enter_context(tc.psum_pool(name="turned", bufs=4))
         output_pool = stack.enter_context(tc.psum_pool(name="output", bufs=1))
         pair_pool = stack.enter_context(tc.psum_pool(name="pair", bufs=3))
 
+        rows_of = {}
+        grouped_of = {}
+        xi_of = {}
+        xi_turned_of = {}
+        xi_grouped_of = {}
+        xi_codes_of = {}
+        xi_scales_of = {}
+        squares_of = {}
+        inverse_of = {}
+        unit_of = {}
+        unit_turned_of = {}
+        unit_grouped_of = {}
+        unit_codes_of = {}
+        unit_scales_of = {}
+
+        def load_rows(g):
+            rows_of[g] = rows_pool.tile([P, PACK, FEATURES], BF16, name="rows")
+            nc.sync.dma_start(
+                out=rows_of[g][:],
+                in_=memory[g * K_PASS : (g + 1) * K_PASS, :].rearrange("(p t) d -> p t d", t=PACK),
+            )
+
+        def load_xi(group):
+            first = group * GROUP * K_PASS
+            xi_of[group] = xi_pool.tile([QUERIES, GROUP * K_PASS], BF16, name="xi_columns")
+            nc.sync.dma_start(out=xi_of[group][:], in_=xi[:, first : first + GROUP * K_PASS])
+
+        load_rows(0)
+        load_xi(0)
+        for g in range(1, AHEAD):
+            load_rows(g)
+        load_xi(1)
+
         identity = consts.tile([P, P], F32)
         make_identity(nc, identity[:])
-
         one = consts.tile([P, 1], F32)
         nc.vector.memset(one[:], 1.0)
         warm = consts.tile([P, 1], F32)
@@ -53,181 +87,257 @@ def tile_hopfieldretrievalmodel_pa_k_kernel(tc, xi, memory, out):
 
         output = output_pool.tile([QUERIES, FEATURES], F32)
 
-        xi_of = {}
-        rows_of = {}
-        inverse_norm_of = {}
-        unit_codes_of = {}
-        unit_scales_of = {}
-
-        def inverse_norm(result, sum_of_squares):
-            nc.vector.tensor_scalar_max(sum_of_squares, sum_of_squares, TINY * TINY)
-            nc.scalar.sqrt(sum_of_squares, sum_of_squares)
-            nc.vector.reciprocal(result, sum_of_squares)
-
-        def load(chunk):
-            first = chunk * CHUNK
-            xi_of[chunk] = xi_pool.tile([QUERIES, CHUNK], BF16, name="xi_columns")
-            rows_of[chunk] = rows_pool.tile([P, PASSES, PACK, FEATURES], BF16, name="rows")
-            source = memory[first : first + CHUNK, :].rearrange(
-                "(g p t) d -> g p t d", g=PASSES, t=PACK
+        def turn_xi(group):
+            words = xi_of[group][:].bitcast(F32).rearrange(
+                "q (g p u) -> q g u p", g=GROUP, u=PAIR
             )
-            nc.sync.dma_start(out=rows_of[chunk][:, 0], in_=source[0])
-            nc.sync.dma_start(out=xi_of[chunk][:], in_=xi[:, first : first + CHUNK])
-            for g in range(1, PASSES):
-                nc.sync.dma_start(out=rows_of[chunk][:, g], in_=source[g])
-
-        def retrieve(chunk):
-            xi_words = xi_of[chunk][:].bitcast(F32).rearrange(
-                "q (g p u) -> q g u p", g=PASSES, u=PAIR
-            )
-            xi_grouped = xi_pool.tile([P, PASSES * QUERIES * PACK], BF16, align_bytes=64)
-            xi_grouped_words = xi_grouped[:].bitcast(F32).rearrange(
-                "p (g q u) -> p g q u", g=PASSES, u=PAIR
-            )
-            for half in range(PASSES // 2):
-                xi_turned = turned_pool.tile([P, 2, PAIR, QUERIES], F32, tag="turned")
-                for g in range(2):
+            for half in range(2):
+                turned = turned_pool.tile([P, 2, PAIR, QUERIES], F32, name="turned")
+                for i in range(2):
                     for u in range(PAIR):
                         nc.tensor.transpose(
-                            xi_turned[:, g, u, :], xi_words[:, 2 * half + g, u, :], identity[:]
+                            turned[:, i, u, :], words[:, 2 * half + i, u, :], identity[:]
                         )
-                nc.vector.tensor_copy(
-                    out=xi_grouped_words[:, 2 * half : 2 * half + 2],
-                    in_=xi_turned[:].rearrange("p g u q -> p g q u"),
-                )
-            xi_codes = xi_pool.tile([P, PASSES * QUERIES], U32, align_bytes=64)
-            xi_scales = xi_pool.tile([P, PASSES * QUERIES], U8, align_bytes=64)
+                xi_turned_of[group, half] = turned
+            xi_grouped_of[group] = xi_pool.tile(
+                [P, GROUP * QUERIES * PACK], BF16, name="xi_grouped", align_bytes=64
+            )
+
+        def group_xi(group, half, copy):
+            words = xi_grouped_of[group][:].bitcast(F32).rearrange(
+                "p (g q u) -> p g q u", g=GROUP, u=PAIR
+            )
+            copy(
+                out=words[:, 2 * half : 2 * half + 2],
+                in_=xi_turned_of[group, half][:].rearrange("p g u q -> p g q u"),
+            )
+
+        def quantise_xi(group):
+            xi_codes_of[group] = xi_pool.tile(
+                [P, GROUP * QUERIES], U32, name="xi_codes", align_bytes=64
+            )
+            xi_scales_of[group] = xi_pool.tile(
+                [P, GROUP * QUERIES], U8, name="xi_scales", align_bytes=64
+            )
             nc.vector.quantize_mx(
-                out=xi_codes[:].bitcast(FP8X4), scales=xi_scales[:], in_=xi_grouped[:]
+                out=xi_codes_of[group][:].bitcast(FP8X4),
+                scales=xi_scales_of[group][:],
+                in_=xi_grouped_of[group][:],
             )
 
-            for g in range(PASSES):
-                grouped = stage.tile([P, FEATURES, PACK], BF16, align_bytes=64)
-                nc.vector.tensor_copy(
-                    out=grouped[:].rearrange("p (c i) t -> p c t i", i=4),
-                    in_=rows_of[chunk][:, g].rearrange("p t (c i) -> p c t i", i=4),
-                )
-                codes = stage.tile([P, FEATURES], U32, align_bytes=64)
-                scales = stage.tile([P, FEATURES], U8, align_bytes=64)
-                nc.vector.quantize_mx(
-                    out=codes[:].bitcast(FP8X4),
-                    scales=scales[:],
-                    in_=grouped[:].rearrange("p d t -> p (d t)"),
-                )
-                queries = slice(g * QUERIES, (g + 1) * QUERIES)
-                nc.tensor.matmul_mx(
-                    out=output[:],
-                    lhsT=xi_codes[:, queries].bitcast(FP8X4),
-                    lhsT_scale=xi_scales[:, queries],
-                    rhs=codes[:].bitcast(FP8X4),
-                    rhs_scale=scales[:],
-                    start=(chunk == 0 and g == 0),
-                    stop=(chunk == CHUNKS - 1 and g == PASSES - 1),
-                )
-
-            sum_of_squares = norm_pool.tile([P, PASSES * PACK], F32)
-            for g in range(PASSES):
-                for t in range(PACK):
-                    squares = stage.tile([P, FEATURES], BF16)
-                    nc.scalar.activation(
-                        out=squares[:],
-                        in_=rows_of[chunk][:, g, t, :],
-                        func=ACT.Square,
-                        accum_out=sum_of_squares[:, g * PACK + t : g * PACK + t + 1],
-                    )
-            inverse_norm_of[chunk] = norm_pool.tile([P, PASSES * PACK], F32, name="inverse_norm")
-            inverse_norm(inverse_norm_of[chunk][:], sum_of_squares[:])
-
-        def turn_and_group(grouped_words, row_words, copy):
-            turned = turned_pool.tile([P, 2, PAIR, P], F32, tag="turned")
-            for i in range(2):
-                for u in range(PAIR):
-                    nc.tensor.transpose(
-                        turned[:, i, u, :], row_words[:, i, u * P : (u + 1) * P], identity[:]
-                    )
-            copy(out=grouped_words, in_=turned[:].rearrange("c i u r -> c i r u"))
-
-        def prepare(chunk):
-            unit_codes_of[chunk] = unit_pool.tile([P, CHUNK], U32, name="unit_codes", align_bytes=64)
-            unit_scales_of[chunk] = unit_pool.tile([P, CHUNK], U8, name="unit_scales", align_bytes=64)
-            for g in range(PASSES):
-                unit = stage.tile([P, PACK, FEATURES], BF16)
-                for t in range(PACK):
-                    nc.vector.tensor_scalar_mul(
-                        out=unit[:, t, :],
-                        in0=rows_of[chunk][:, g, t, :],
-                        scalar1=inverse_norm_of[chunk][:, g * PACK + t : g * PACK + t + 1],
-                    )
-                unit_grouped = stage.tile([P, K_PASS * PACK], BF16, align_bytes=64)
-                unit_grouped_words = unit_grouped[:].bitcast(F32).rearrange(
-                    "c (t p u) -> c t p u", t=PACK, u=PAIR
-                )
-                unit_words = unit[:].bitcast(F32)
-                for half in range(PACK // 2):
-                    both = slice(2 * half, 2 * half + 2)
-                    turn_and_group(unit_grouped_words[:, both], unit_words[:, both], nc.scalar.copy)
-                columns = slice(g * K_PASS, (g + 1) * K_PASS)
-                nc.vector.quantize_mx(
-                    out=unit_codes_of[chunk][:, columns].bitcast(FP8X4),
-                    scales=unit_scales_of[chunk][:, columns],
-                    in_=unit_grouped[:],
-                )
-
-        def normalise_output():
-            squares = stage.tile([QUERIES, FEATURES], BF16)
-            sum_of_squares = consts.tile([QUERIES, 1], F32, name="output_sum_of_squares")
-            nc.scalar.activation(
-                out=squares[:], in_=output[:], func=ACT.Square, accum_out=sum_of_squares[:]
-            )
-            inverse = consts.tile([QUERIES, 1], F32, name="output_inverse_norm")
-            inverse_norm(inverse[:], sum_of_squares[:])
-            unit = consts.tile([QUERIES, FEATURES], BF16, name="unit_output")
-            nc.vector.tensor_scalar_mul(out=unit[:], in0=output[:], scalar1=inverse[:])
-            unit_words = unit[:].bitcast(F32)
-            turned = turned_pool.tile([P, PAIR, QUERIES], F32, tag="turned")
-            for u in range(PAIR):
-                nc.tensor.transpose(turned[:, u, :], unit_words[:, u * P : (u + 1) * P], identity[:])
-            grouped = consts.tile([P, QUERIES * PACK], BF16, name="unit_output_grouped", align_bytes=64)
+        def group_patterns(g):
+            grouped_of[g] = stage.tile([P, FEATURES, PACK], BF16, name="grouped", align_bytes=64)
             nc.vector.tensor_copy(
-                out=grouped[:].bitcast(F32).rearrange("c (q u) -> c q u", u=PAIR),
-                in_=turned[:].rearrange("c u q -> c q u"),
+                out=grouped_of[g][:].rearrange("p (c i) t -> p c t i", i=4),
+                in_=rows_of[g][:].rearrange("p t (c i) -> p c t i", i=4),
             )
-            codes = consts.tile([P, QUERIES], U32, name="unit_output_codes", align_bytes=64)
-            scales = consts.tile([P, QUERIES], U8, name="unit_output_scales", align_bytes=64)
-            nc.vector.quantize_mx(out=codes[:].bitcast(FP8X4), scales=scales[:], in_=grouped[:])
-            return codes, scales
 
-        def cosines(chunk, output_codes, output_scales):
-            for g in range(PASSES):
-                columns = slice(g * K_PASS, (g + 1) * K_PASS)
-                pair = pair_pool.tile([QUERIES, K_PASS], F32)
-                nc.tensor.matmul_mx(
-                    out=pair[:],
-                    lhsT=output_codes[:].bitcast(FP8X4),
-                    lhsT_scale=output_scales[:],
-                    rhs=unit_codes_of[chunk][:, columns].bitcast(FP8X4),
-                    rhs_scale=unit_scales_of[chunk][:, columns],
-                    start=True,
-                    stop=True,
-                )
-                ordered = stage.tile([QUERIES, K_PASS], F32)
-                copy = nc.scalar.copy if g == PASSES - 1 else nc.vector.tensor_copy
-                copy(
-                    out=ordered[:].rearrange("q (p t) -> q p t", t=PACK),
-                    in_=pair[:].rearrange("q (t p) -> q p t", t=PACK),
-                )
-                first = chunk * CHUNK + g * K_PASS
-                nc.sync.dma_start(out=out[:, first : first + K_PASS], in_=ordered[:])
+        def retrieve(g):
+            codes = stage.tile([P, FEATURES], U32, name="codes", align_bytes=64)
+            scales = stage.tile([P, FEATURES], U8, name="scales", align_bytes=64)
+            nc.vector.quantize_mx(
+                out=codes[:].bitcast(FP8X4),
+                scales=scales[:],
+                in_=grouped_of[g][:].rearrange("p d t -> p (d t)"),
+            )
+            group, place = divmod(g, GROUP)
+            queries = slice(place * QUERIES, (place + 1) * QUERIES)
+            nc.tensor.matmul_mx(
+                out=output[:],
+                lhsT=xi_codes_of[group][:, queries].bitcast(FP8X4),
+                lhsT_scale=xi_scales_of[group][:, queries],
+                rhs=codes[:].bitcast(FP8X4),
+                rhs_scale=scales[:],
+                start=(g == 0),
+                stop=(g == PASSES - 1),
+            )
 
-        load(0)
-        for chunk in range(CHUNKS):
-            if chunk + 1 < CHUNKS:
-                load(chunk + 1)
-            retrieve(chunk)
-            if chunk >= LAG:
-                prepare(chunk - LAG)
-        output_codes, output_scales = normalise_output()
-        for chunk in range(CHUNKS):
-            if chunk >= CHUNKS - LAG:
-                prepare(chunk)
-            cosines(chunk, output_codes, output_scales)
+        def square_row(g, t):
+            group, place = divmod(g, GROUP)
+            if place == 0 and t == 0:
+                squares_of[group] = norm_pool.tile([P, GROUP * PACK], F32, name="sum_of_squares")
+            squares = stage.tile([P, FEATURES], BF16, name="squares")
+            column = place * PACK + t
+            nc.scalar.activation(
+                out=squares[:],
+                in_=rows_of[g][:, t, :],
+                func=ACT.Square,
+                accum_out=squares_of[group][:, column : column + 1],
+            )
+
+        def clamp(sums):
+            nc.vector.tensor_scalar_max(sums, sums, TINY * TINY)
+
+        def invert(group):
+            inverse_of[group] = norm_pool.tile([P, GROUP * PACK], F32, name="inverse_norm")
+            nc.vector.reciprocal(inverse_of[group][:], squares_of[group][:])
+
+        def scale_rows(g):
+            group, place = divmod(g, GROUP)
+            unit_of[g] = stage.tile([P, PACK, FEATURES], BF16, name="unit")
+            for t in range(PACK):
+                column = place * PACK + t
+                nc.vector.tensor_scalar_mul(
+                    out=unit_of[g][:, t, :],
+                    in0=rows_of[g][:, t, :],
+                    scalar1=inverse_of[group][:, column : column + 1],
+                )
+
+        def turn_rows(g):
+            words = unit_of[g][:].bitcast(F32)
+            for half in range(2):
+                turned = turned_pool.tile([P, 2, PAIR, P], F32, name="turned")
+                for i in range(2):
+                    for u in range(PAIR):
+                        nc.tensor.transpose(
+                            turned[:, i, u, :],
+                            words[:, 2 * half + i, u * P : (u + 1) * P],
+                            identity[:],
+                        )
+                unit_turned_of[g, half] = turned
+            unit_grouped_of[g] = stage.tile(
+                [P, K_PASS * PACK], BF16, name="unit_grouped", align_bytes=64
+            )
+
+        def group_features(g, half):
+            words = unit_grouped_of[g][:].bitcast(F32).rearrange(
+                "c (t p u) -> c t p u", t=PACK, u=PAIR
+            )
+            nc.scalar.copy(
+                out=words[:, 2 * half : 2 * half + 2],
+                in_=unit_turned_of[g, half][:].rearrange("c i u r -> c i r u"),
+            )
+
+        def quantise_rows(g):
+            unit_codes_of[g] = unit_pool.tile([P, K_PASS], U32, name="unit_codes", align_bytes=64)
+            unit_scales_of[g] = unit_pool.tile([P, K_PASS], U8, name="unit_scales", align_bytes=64)
+            nc.vector.quantize_mx(
+                out=unit_codes_of[g][:].bitcast(FP8X4),
+                scales=unit_scales_of[g][:],
+                in_=unit_grouped_of[g][:],
+            )
+
+        output_squares = consts.tile([QUERIES, FEATURES], BF16)
+        output_norm = consts.tile([QUERIES, 1], F32)
+        output_inverse = consts.tile([QUERIES, 1], F32)
+        output_unit = consts.tile([QUERIES, FEATURES], BF16)
+        output_grouped = consts.tile([P, QUERIES * PACK], BF16, align_bytes=64)
+        output_codes = consts.tile([P, QUERIES], U32, align_bytes=64)
+        output_scales = consts.tile([P, QUERIES], U8, align_bytes=64)
+
+        def cosines(g):
+            pair = pair_pool.tile([QUERIES, K_PASS], F32)
+            nc.tensor.matmul_mx(
+                out=pair[:],
+                lhsT=output_codes[:].bitcast(FP8X4),
+                lhsT_scale=output_scales[:],
+                rhs=unit_codes_of[g][:].bitcast(FP8X4),
+                rhs_scale=unit_scales_of[g][:],
+                start=True,
+                stop=True,
+            )
+            ordered = store_pool.tile([QUERIES, K_PASS], F32)
+            copy = nc.vector.tensor_copy if g % 2 else nc.scalar.copy
+            copy(
+                out=ordered[:].rearrange("q (p t) -> q p t", t=PACK),
+                in_=pair[:].rearrange("q (t p) -> q p t", t=PACK),
+            )
+            nc.sync.dma_start(out=out[:, g * K_PASS : (g + 1) * K_PASS], in_=ordered[:])
+
+        STEPS = PASSES + LAG + 1
+        FIRST_COSINES = PASSES + 2
+        done = 0
+
+        with tc.manual_schedule():
+            for step in range(STEPS):
+                group, place = divmod(step, GROUP)
+                u = step - LAG
+
+                if step + AHEAD < PASSES:
+                    load_rows(step + AHEAD)
+                if place == 0 and group + 2 < GROUPS:
+                    load_xi(group + 2)
+
+                if 0 <= u < PASSES:
+                    scale_rows(u)
+
+                if step == PASSES + 1:
+                    clamp(output_norm[:])
+                    nc.scalar.sqrt(output_norm[:], output_norm[:])
+                    nc.vector.reciprocal(output_inverse[:], output_norm[:])
+                    nc.scalar.activation(
+                        out=output_unit[:], in_=output[:], func=ACT.Copy, scale=output_inverse[:]
+                    )
+                    turned = turned_pool.tile([P, PAIR, QUERIES], F32, name="turned")
+                    words = output_unit[:].bitcast(F32)
+                    for w in range(PAIR):
+                        nc.tensor.transpose(
+                            turned[:, w, :], words[:, w * P : (w + 1) * P], identity[:]
+                        )
+                    nc.scalar.copy(
+                        out=output_grouped[:].bitcast(F32).rearrange("c (q u) -> c q u", u=PAIR),
+                        in_=turned[:].rearrange("c u q -> c q u"),
+                    )
+                if step == FIRST_COSINES:
+                    nc.vector.quantize_mx(
+                        out=output_codes[:].bitcast(FP8X4),
+                        scales=output_scales[:],
+                        in_=output_grouped[:],
+                    )
+
+                if step == STEPS - 1:
+                    quantise_rows(u - 1)
+                if step >= FIRST_COSINES:
+                    due = PASSES * (step - FIRST_COSINES + 1) // (STEPS - FIRST_COSINES)
+                    for g in range(done, due):
+                        cosines(g)
+                    done = due
+
+                if 0 <= u < PASSES:
+                    turn_rows(u)
+                if 1 <= step <= PASSES:
+                    retrieve(step - 1)
+                if step < PASSES:
+                    group_patterns(step)
+                    square_row(step, 0)
+                    square_row(step, 1)
+                if 0 <= u < PASSES:
+                    group_features(u, 0)
+                if step < PASSES:
+                    square_row(step, 2)
+                if 0 <= u < PASSES:
+                    group_features(u, 1)
+                if step < PASSES:
+                    square_row(step, 3)
+                if step == PASSES:
+                    nc.scalar.activation(
+                        out=output_squares[:],
+                        in_=output[:],
+                        func=ACT.Square,
+                        accum_out=output_norm[:],
+                    )
+
+                if step == 0:
+                    turn_xi(0)
+                    group_xi(0, 0, nc.vector.tensor_copy)
+                    group_xi(0, 1, nc.scalar.copy)
+                    quantise_xi(0)
+                if group + 1 < GROUPS:
+                    if place == 1:
+                        turn_xi(group + 1)
+                        group_xi(group + 1, 0, nc.vector.tensor_copy)
+                    if place == 2:
+                        group_xi(group + 1, 1, nc.scalar.copy)
+                    if place == 3:
+                        quantise_xi(group + 1)
+
+                if 1 <= u < PASSES:
+                    quantise_rows(u - 1)
+
+                if 1 <= group <= GROUPS:
+                    if place == 0:
+                        clamp(squares_of[group - 1][:])
+                    if place == 1:
+                        nc.scalar.sqrt(squares_of[group - 1][:], squares_of[group - 1][:])
+                    if place == 2:
+                        invert(group - 1)

@@ -41,9 +41,8 @@ def tile_hopfieldretrievalmodel_pa_k_kernel(tc, xi, memory, out):
         xi_pool = stack.enter_context(tc.tile_pool(name="xi", bufs=3))
         stage = stack.enter_context(tc.tile_pool(name="stage", bufs=3))
         store_pool = stack.enter_context(tc.tile_pool(name="store", bufs=6))
-        turned_pool = stack.enter_context(tc.psum_pool(name="turned", bufs=4))
         output_pool = stack.enter_context(tc.psum_pool(name="output", bufs=1))
-        pair_pool = stack.enter_context(tc.psum_pool(name="pair", bufs=3))
+        bank_pool = stack.enter_context(tc.psum_pool(name="bank", bufs=7))
 
         rows_of = {}
         grouped_of = {}
@@ -62,10 +61,12 @@ def tile_hopfieldretrievalmodel_pa_k_kernel(tc, xi, memory, out):
 
         def load_rows(g):
             rows_of[g] = rows_pool.tile([P, PACK, FEATURES], BF16, name="rows")
-            nc.sync.dma_start(
-                out=rows_of[g][:],
-                in_=memory[g * K_PASS : (g + 1) * K_PASS, :].rearrange("(p t) d -> p t d", t=PACK),
-            )
+            source = memory[g * K_PASS : (g + 1) * K_PASS, :].rearrange("(p t) d -> p t d", t=PACK)
+            pieces = PACK if g == 0 else 1
+            size = PACK // pieces
+            for i in range(pieces):
+                piece = slice(i * size, (i + 1) * size)
+                nc.sync.dma_start(out=rows_of[g][:, piece, :], in_=source[:, piece, :])
 
         def load_xi(group):
             first = group * GROUP * K_PASS
@@ -92,7 +93,7 @@ def tile_hopfieldretrievalmodel_pa_k_kernel(tc, xi, memory, out):
                 "q (g p u) -> q g u p", g=GROUP, u=PAIR
             )
             for half in range(2):
-                turned = turned_pool.tile([P, 2, PAIR, QUERIES], F32, name="turned")
+                turned = bank_pool.tile([P, 2, PAIR, QUERIES], F32, name="bank")
                 for i in range(2):
                     for u in range(PAIR):
                         nc.tensor.transpose(
@@ -168,10 +169,6 @@ def tile_hopfieldretrievalmodel_pa_k_kernel(tc, xi, memory, out):
         def clamp(sums):
             nc.vector.tensor_scalar_max(sums, sums, TINY * TINY)
 
-        def invert(group):
-            inverse_of[group] = norm_pool.tile([P, GROUP * PACK], F32, name="inverse_norm")
-            nc.vector.reciprocal(inverse_of[group][:], squares_of[group][:])
-
         def scale_rows(g):
             group, place = divmod(g, GROUP)
             unit_of[g] = stage.tile([P, PACK, FEATURES], BF16, name="unit")
@@ -186,7 +183,7 @@ def tile_hopfieldretrievalmodel_pa_k_kernel(tc, xi, memory, out):
         def turn_rows(g):
             words = unit_of[g][:].bitcast(F32)
             for half in range(2):
-                turned = turned_pool.tile([P, 2, PAIR, P], F32, name="turned")
+                turned = bank_pool.tile([P, 2, PAIR, P], F32, name="bank")
                 for i in range(2):
                     for u in range(PAIR):
                         nc.tensor.transpose(
@@ -226,7 +223,7 @@ def tile_hopfieldretrievalmodel_pa_k_kernel(tc, xi, memory, out):
         output_scales = consts.tile([P, QUERIES], U8, align_bytes=64)
 
         def cosines(g):
-            pair = pair_pool.tile([QUERIES, K_PASS], F32)
+            pair = bank_pool.tile([QUERIES, K_PASS], F32, name="bank")
             nc.tensor.matmul_mx(
                 out=pair[:],
                 lhsT=output_codes[:].bitcast(FP8X4),
@@ -245,7 +242,7 @@ def tile_hopfieldretrievalmodel_pa_k_kernel(tc, xi, memory, out):
             nc.sync.dma_start(out=out[:, g * K_PASS : (g + 1) * K_PASS], in_=ordered[:])
 
         STEPS = PASSES + LAG + 1
-        FIRST_COSINES = PASSES + 2
+        FIRST_COSINES = PASSES + 3
         done = 0
 
         with tc.manual_schedule():
@@ -260,15 +257,53 @@ def tile_hopfieldretrievalmodel_pa_k_kernel(tc, xi, memory, out):
 
                 if 0 <= u < PASSES:
                     scale_rows(u)
-
                 if step == PASSES + 1:
                     clamp(output_norm[:])
+                if step > PASSES:
+                    quantise_rows(u - 1)
+                if step == FIRST_COSINES - 1:
+                    nc.vector.quantize_mx(
+                        out=output_codes[:].bitcast(FP8X4),
+                        scales=output_scales[:],
+                        in_=output_grouped[:],
+                    )
+                if step >= FIRST_COSINES:
+                    due = PASSES * (step - FIRST_COSINES + 1) // (STEPS - FIRST_COSINES)
+                    for g in range(done, due):
+                        cosines(g)
+                    done = due
+                if 0 <= u < PASSES:
+                    turn_rows(u)
+                if step < PASSES:
+                    group_patterns(step)
+                    square_row(step, 0)
+                    square_row(step, 1)
+                if 1 <= step <= PASSES:
+                    retrieve(step - 1)
+                if 0 <= u < PASSES:
+                    group_features(u, 0)
+                if step < PASSES:
+                    square_row(step, 2)
+                if step == PASSES + 1:
                     nc.scalar.sqrt(output_norm[:], output_norm[:])
                     nc.vector.reciprocal(output_inverse[:], output_norm[:])
+                if 0 <= u < PASSES:
+                    group_features(u, 1)
+                if step < PASSES:
+                    square_row(step, 3)
+
+                if step == PASSES:
+                    nc.scalar.activation(
+                        out=output_squares[:],
+                        in_=output[:],
+                        func=ACT.Square,
+                        accum_out=output_norm[:],
+                    )
+                if step == PASSES + 1:
                     nc.scalar.activation(
                         out=output_unit[:], in_=output[:], func=ACT.Copy, scale=output_inverse[:]
                     )
-                    turned = turned_pool.tile([P, PAIR, QUERIES], F32, name="turned")
+                    turned = bank_pool.tile([P, PAIR, QUERIES], F32, name="bank")
                     words = output_unit[:].bitcast(F32)
                     for w in range(PAIR):
                         nc.tensor.transpose(
@@ -278,66 +313,32 @@ def tile_hopfieldretrievalmodel_pa_k_kernel(tc, xi, memory, out):
                         out=output_grouped[:].bitcast(F32).rearrange("c (q u) -> c q u", u=PAIR),
                         in_=turned[:].rearrange("c u q -> c q u"),
                     )
-                if step == FIRST_COSINES:
-                    nc.vector.quantize_mx(
-                        out=output_codes[:].bitcast(FP8X4),
-                        scales=output_scales[:],
-                        in_=output_grouped[:],
-                    )
-
-                if step == STEPS - 1:
-                    quantise_rows(u - 1)
-                if step >= FIRST_COSINES:
-                    due = PASSES * (step - FIRST_COSINES + 1) // (STEPS - FIRST_COSINES)
-                    for g in range(done, due):
-                        cosines(g)
-                    done = due
-
-                if 0 <= u < PASSES:
-                    turn_rows(u)
-                if 1 <= step <= PASSES:
-                    retrieve(step - 1)
-                if step < PASSES:
-                    group_patterns(step)
-                    square_row(step, 0)
-                    square_row(step, 1)
-                if 0 <= u < PASSES:
-                    group_features(u, 0)
-                if step < PASSES:
-                    square_row(step, 2)
-                if 0 <= u < PASSES:
-                    group_features(u, 1)
-                if step < PASSES:
-                    square_row(step, 3)
-                if step == PASSES:
-                    nc.scalar.activation(
-                        out=output_squares[:],
-                        in_=output[:],
-                        func=ACT.Square,
-                        accum_out=output_norm[:],
-                    )
 
                 if step == 0:
                     turn_xi(0)
                     group_xi(0, 0, nc.vector.tensor_copy)
-                    group_xi(0, 1, nc.scalar.copy)
+                    group_xi(0, 1, nc.vector.tensor_copy)
                     quantise_xi(0)
                 if group + 1 < GROUPS:
-                    if place == 1:
+                    if place == 0:
                         turn_xi(group + 1)
+                    if place == 1:
                         group_xi(group + 1, 0, nc.vector.tensor_copy)
                     if place == 2:
-                        group_xi(group + 1, 1, nc.scalar.copy)
+                        group_xi(group + 1, 1, nc.vector.tensor_copy)
                     if place == 3:
                         quantise_xi(group + 1)
 
-                if 1 <= u < PASSES:
+                if 1 <= u and step <= PASSES:
                     quantise_rows(u - 1)
 
                 if 1 <= group <= GROUPS:
+                    sums = squares_of[group - 1]
                     if place == 0:
-                        clamp(squares_of[group - 1][:])
+                        clamp(sums[:])
                     if place == 1:
-                        nc.scalar.sqrt(squares_of[group - 1][:], squares_of[group - 1][:])
+                        nc.scalar.sqrt(sums[:], sums[:])
                     if place == 2:
-                        invert(group - 1)
+                        inverse = norm_pool.tile([P, GROUP * PACK], F32, name="inverse_norm")
+                        nc.vector.reciprocal(inverse[:], sums[:])
+                        inverse_of[group - 1] = inverse

@@ -24,6 +24,7 @@ PASSES = PATTERNS // K_PASS
 GROUP = 4
 GROUPS = PASSES // GROUP
 LAG = 14
+RUN = 8
 AHEAD = 4
 
 FLOPS = 2 * 2 * QUERIES * PATTERNS * FEATURES
@@ -129,8 +130,8 @@ def tile_hopfieldretrievalmodel_pa_k_kernel(tc, xi, memory, out):
         def group_patterns(g):
             grouped_of[g] = stage.tile([P, FEATURES, PACK], BF16, name="grouped", align_bytes=64)
             nc.vector.tensor_copy(
-                out=grouped_of[g][:].rearrange("p (c i) t -> p c t i", i=4),
-                in_=rows_of[g][:].rearrange("p t (c i) -> p c t i", i=4),
+                out=grouped_of[g][:].rearrange("p (c i) t -> p c t i", i=RUN),
+                in_=rows_of[g][:].rearrange("p t (c i) -> p c t i", i=RUN),
             )
 
         def retrieve(g):

@@ -89,23 +89,23 @@ def tile_hopfieldretrievalmodel_pa_k_kernel(tc, xi, memory, out):
 
         output = output_pool.tile([QUERIES, FEATURES], F32)
 
-        def turn_xi(group):
+        def turn_xi(group, half):
             words = xi_of[group][:].bitcast(F32).rearrange(
                 "q (g p u) -> q g u p", g=GROUP, u=PAIR
             )
-            for half in range(2):
-                turned = bank_pool.tile([P, 2, PAIR, QUERIES], F32, name="bank")
-                for i in range(2):
-                    for u in range(PAIR):
-                        nc.tensor.transpose(
-                            turned[:, i, u, :], words[:, 2 * half + i, u, :], identity[:]
-                        )
-                xi_turned_of[group, half] = turned
-            xi_grouped_of[group] = xi_pool.tile(
-                [P, GROUP * QUERIES * PACK], BF16, name="xi_grouped", align_bytes=64
-            )
+            turned = bank_pool.tile([P, 2, PAIR, QUERIES], F32, name="bank")
+            for i in range(2):
+                for u in range(PAIR):
+                    nc.tensor.transpose(
+                        turned[:, i, u, :], words[:, 2 * half + i, u, :], identity[:]
+                    )
+            xi_turned_of[group, half] = turned
 
         def group_xi(group, half, copy):
+            if half == 0:
+                xi_grouped_of[group] = xi_pool.tile(
+                    [P, GROUP * QUERIES * PACK], BF16, name="xi_grouped", align_bytes=64
+                )
             words = xi_grouped_of[group][:].bitcast(F32).rearrange(
                 "p (g q u) -> p g q u", g=GROUP, u=PAIR
             )
@@ -260,8 +260,11 @@ def tile_hopfieldretrievalmodel_pa_k_kernel(tc, xi, memory, out):
                     scale_rows(u)
                 if step == PASSES + 1:
                     clamp(output_norm[:])
-                if step > PASSES:
+                    nc.scalar.sqrt(output_norm[:], output_norm[:])
+                if PASSES < step < FIRST_COSINES:
                     quantise_rows(u - 1)
+                if step == PASSES + 1:
+                    nc.vector.reciprocal(output_inverse[:], output_norm[:])
                 if step == FIRST_COSINES - 1:
                     nc.vector.quantize_mx(
                         out=output_codes[:].bitcast(FP8X4),
@@ -270,11 +273,19 @@ def tile_hopfieldretrievalmodel_pa_k_kernel(tc, xi, memory, out):
                     )
                 if step >= FIRST_COSINES:
                     due = PASSES * (step - FIRST_COSINES + 1) // (STEPS - FIRST_COSINES)
-                    for g in range(done, due):
+                    for g in range(done, min(due, u - 1)):
+                        cosines(g)
+                    quantise_rows(u - 1)
+                    for g in range(max(done, u - 1), due):
                         cosines(g)
                     done = due
                 if 0 <= u < PASSES:
                     turn_rows(u)
+                if step == 0:
+                    for half in range(2):
+                        turn_xi(0, half)
+                if place < 2 and group + 1 < GROUPS:
+                    turn_xi(group + 1, place)
                 if step < PASSES:
                     group_patterns(step)
                     square_row(step, 0)
@@ -285,9 +296,6 @@ def tile_hopfieldretrievalmodel_pa_k_kernel(tc, xi, memory, out):
                     group_features(u, 0)
                 if step < PASSES:
                     square_row(step, 2)
-                if step == PASSES + 1:
-                    nc.scalar.sqrt(output_norm[:], output_norm[:])
-                    nc.vector.reciprocal(output_inverse[:], output_norm[:])
                 if 0 <= u < PASSES:
                     group_features(u, 1)
                 if step < PASSES:
@@ -316,17 +324,12 @@ def tile_hopfieldretrievalmodel_pa_k_kernel(tc, xi, memory, out):
                     )
 
                 if step == 0:
-                    turn_xi(0)
-                    group_xi(0, 0, nc.vector.tensor_copy)
-                    group_xi(0, 1, nc.vector.tensor_copy)
+                    for half in range(2):
+                        group_xi(0, half, nc.vector.tensor_copy)
                     quantise_xi(0)
                 if group + 1 < GROUPS:
-                    if place == 0:
-                        turn_xi(group + 1)
-                    if place == 1:
-                        group_xi(group + 1, 0, nc.vector.tensor_copy)
-                    if place == 2:
-                        group_xi(group + 1, 1, nc.vector.tensor_copy)
+                    if 1 <= place <= 2:
+                        group_xi(group + 1, place - 1, nc.vector.tensor_copy)
                     if place == 3:
                         quantise_xi(group + 1)
 

@@ -36,12 +36,13 @@ def tile_hopfieldretrievalmodel_pa_k_kernel(tc, xi, memory, out):
     nc = tc.nc
     with ExitStack() as stack:
         consts = stack.enter_context(tc.tile_pool(name="consts", bufs=1))
-        rows_pool = stack.enter_context(tc.tile_pool(name="rows", bufs=LAG + AHEAD + 2))
+        rows_pool = stack.enter_context(tc.tile_pool(name="rows", bufs=LAG + AHEAD + 3))
         unit_pool = stack.enter_context(tc.tile_pool(name="unit", bufs=PASSES - LAG + 3))
         norm_pool = stack.enter_context(tc.tile_pool(name="norm", bufs=LAG // GROUP + 3))
         xi_pool = stack.enter_context(tc.tile_pool(name="xi", bufs=3))
         stage = stack.enter_context(tc.tile_pool(name="stage", bufs=3))
-        store_pool = stack.enter_context(tc.tile_pool(name="store", bufs=6))
+        codes_pool = stack.enter_context(tc.tile_pool(name="codes", bufs=6))
+        store_pool = stack.enter_context(tc.tile_pool(name="store", bufs=12))
         output_pool = stack.enter_context(tc.psum_pool(name="output", bufs=1))
         bank_pool = stack.enter_context(tc.psum_pool(name="bank", bufs=7))
 
@@ -54,14 +55,12 @@ def tile_hopfieldretrievalmodel_pa_k_kernel(tc, xi, memory, out):
         xi_scales_of = {}
         squares_of = {}
         inverse_of = {}
-        unit_of = {}
         unit_turned_of = {}
-        unit_grouped_of = {}
         unit_codes_of = {}
         unit_scales_of = {}
 
         def load_rows(g):
-            rows_of[g] = rows_pool.tile([P, PACK, FEATURES], BF16, name="rows")
+            rows_of[g] = rows_pool.tile([P, PACK, FEATURES], BF16, name="rows", align_bytes=64)
             source = memory[g * K_PASS : (g + 1) * K_PASS, :].rearrange("(p t) d -> p t d", t=PACK)
             pieces = PACK if g == 0 else 1
             size = PACK // pieces
@@ -135,8 +134,8 @@ def tile_hopfieldretrievalmodel_pa_k_kernel(tc, xi, memory, out):
             )
 
         def retrieve(g):
-            codes = stage.tile([P, FEATURES], U32, name="codes", align_bytes=64)
-            scales = stage.tile([P, FEATURES], U8, name="scales", align_bytes=64)
+            codes = codes_pool.tile([P, FEATURES], U32, name="codes", align_bytes=64)
+            scales = codes_pool.tile([P, FEATURES], U8, name="scales", align_bytes=64)
             nc.vector.quantize_mx(
                 out=codes[:].bitcast(FP8X4),
                 scales=scales[:],
@@ -172,17 +171,16 @@ def tile_hopfieldretrievalmodel_pa_k_kernel(tc, xi, memory, out):
 
         def scale_rows(g):
             group, place = divmod(g, GROUP)
-            unit_of[g] = stage.tile([P, PACK, FEATURES], BF16, name="unit")
             for t in range(PACK):
                 column = place * PACK + t
                 nc.vector.tensor_scalar_mul(
-                    out=unit_of[g][:, t, :],
+                    out=rows_of[g][:, t, :],
                     in0=rows_of[g][:, t, :],
                     scalar1=inverse_of[group][:, column : column + 1],
                 )
 
         def turn_rows(g):
-            words = unit_of[g][:].bitcast(F32)
+            words = rows_of[g][:].bitcast(F32)
             for half in range(2):
                 turned = bank_pool.tile([P, 2, PAIR, P], F32, name="bank")
                 for i in range(2):
@@ -193,14 +191,9 @@ def tile_hopfieldretrievalmodel_pa_k_kernel(tc, xi, memory, out):
                             identity[:],
                         )
                 unit_turned_of[g, half] = turned
-            unit_grouped_of[g] = stage.tile(
-                [P, K_PASS * PACK], BF16, name="unit_grouped", align_bytes=64
-            )
 
         def group_features(g, half):
-            words = unit_grouped_of[g][:].bitcast(F32).rearrange(
-                "c (t p u) -> c t p u", t=PACK, u=PAIR
-            )
+            words = rows_of[g][:].bitcast(F32).rearrange("c t (p u) -> c t p u", u=PAIR)
             nc.scalar.copy(
                 out=words[:, 2 * half : 2 * half + 2],
                 in_=unit_turned_of[g, half][:].rearrange("c i u r -> c i r u"),
@@ -212,7 +205,7 @@ def tile_hopfieldretrievalmodel_pa_k_kernel(tc, xi, memory, out):
             nc.vector.quantize_mx(
                 out=unit_codes_of[g][:].bitcast(FP8X4),
                 scales=unit_scales_of[g][:],
-                in_=unit_grouped_of[g][:],
+                in_=rows_of[g][:].rearrange("c t d -> c (t d)"),
             )
 
         output_squares = consts.tile([QUERIES, FEATURES], BF16)

@@ -25,7 +25,7 @@ GROUP = 4
 GROUPS = PASSES // GROUP
 LAG = 14
 RUN = 8
-AHEAD = 4
+AHEAD = 3
 
 FLOPS = 2 * 2 * QUERIES * PATTERNS * FEATURES
 
@@ -40,9 +40,10 @@ def tile_hopfieldretrievalmodel_pa_k_kernel(tc, xi, memory, out):
         unit_pool = stack.enter_context(tc.tile_pool(name="unit", bufs=PASSES - LAG + 3))
         norm_pool = stack.enter_context(tc.tile_pool(name="norm", bufs=LAG // GROUP + 3))
         xi_pool = stack.enter_context(tc.tile_pool(name="xi", bufs=3))
-        stage = stack.enter_context(tc.tile_pool(name="stage", bufs=3))
+        grouped_pool = stack.enter_context(tc.tile_pool(name="grouped", bufs=4))
         codes_pool = stack.enter_context(tc.tile_pool(name="codes", bufs=6))
-        store_pool = stack.enter_context(tc.tile_pool(name="store", bufs=12))
+        squares_pool = stack.enter_context(tc.tile_pool(name="squares", bufs=16))
+        store_pool = stack.enter_context(tc.tile_pool(name="store", bufs=4))
         output_pool = stack.enter_context(tc.psum_pool(name="output", bufs=1))
         bank_pool = stack.enter_context(tc.psum_pool(name="bank", bufs=7))
 
@@ -127,7 +128,7 @@ def tile_hopfieldretrievalmodel_pa_k_kernel(tc, xi, memory, out):
             )
 
         def group_patterns(g):
-            grouped_of[g] = stage.tile([P, FEATURES, PACK], BF16, name="grouped", align_bytes=64)
+            grouped_of[g] = grouped_pool.tile([P, FEATURES, PACK], BF16, name="grouped", align_bytes=64)
             nc.vector.tensor_copy(
                 out=grouped_of[g][:].rearrange("p (c i) t -> p c t i", i=RUN),
                 in_=rows_of[g][:].rearrange("p t (c i) -> p c t i", i=RUN),
@@ -157,7 +158,7 @@ def tile_hopfieldretrievalmodel_pa_k_kernel(tc, xi, memory, out):
             group, place = divmod(g, GROUP)
             if place == 0 and t == 0:
                 squares_of[group] = norm_pool.tile([P, GROUP * PACK], F32, name="sum_of_squares")
-            squares = stage.tile([P, FEATURES], BF16, name="squares")
+            squares = squares_pool.tile([P, FEATURES], BF16, name="squares")
             column = place * PACK + t
             nc.scalar.activation(
                 out=squares[:],
@@ -192,9 +193,9 @@ def tile_hopfieldretrievalmodel_pa_k_kernel(tc, xi, memory, out):
                         )
                 unit_turned_of[g, half] = turned
 
-        def group_features(g, half):
+        def group_features(g, half, copy):
             words = rows_of[g][:].bitcast(F32).rearrange("c t (p u) -> c t p u", u=PAIR)
-            nc.scalar.copy(
+            copy(
                 out=words[:, 2 * half : 2 * half + 2],
                 in_=unit_turned_of[g, half][:].rearrange("c i u r -> c i r u"),
             )
@@ -216,27 +217,31 @@ def tile_hopfieldretrievalmodel_pa_k_kernel(tc, xi, memory, out):
         output_codes = consts.tile([P, QUERIES], U32, align_bytes=64)
         output_scales = consts.tile([P, QUERIES], U8, align_bytes=64)
 
-        def cosines(g):
-            pair = bank_pool.tile([QUERIES, K_PASS], F32, name="bank")
-            nc.tensor.matmul_mx(
-                out=pair[:],
-                lhsT=output_codes[:].bitcast(FP8X4),
-                lhsT_scale=output_scales[:],
-                rhs=unit_codes_of[g][:].bitcast(FP8X4),
-                rhs_scale=unit_scales_of[g][:],
-                start=True,
-                stop=True,
+        def cosines(first, last, copy):
+            ordered = store_pool.tile([QUERIES, last - first, K_PASS], F32, name="ordered")
+            for g in range(first, last):
+                pair = bank_pool.tile([QUERIES, K_PASS], F32, name="bank")
+                nc.tensor.matmul_mx(
+                    out=pair[:],
+                    lhsT=output_codes[:].bitcast(FP8X4),
+                    lhsT_scale=output_scales[:],
+                    rhs=unit_codes_of[g][:].bitcast(FP8X4),
+                    rhs_scale=unit_scales_of[g][:],
+                    start=True,
+                    stop=True,
+                )
+                copy(
+                    out=ordered[:, g - first, :].rearrange("q (p t) -> q p t", t=PACK),
+                    in_=pair[:].rearrange("q (t p) -> q p t", t=PACK),
+                )
+            nc.sync.dma_start(
+                out=out[:, first * K_PASS : last * K_PASS],
+                in_=ordered[:].rearrange("q g k -> q (g k)"),
             )
-            ordered = store_pool.tile([QUERIES, K_PASS], F32)
-            copy = nc.vector.tensor_copy if g % 2 else nc.scalar.copy
-            copy(
-                out=ordered[:].rearrange("q (p t) -> q p t", t=PACK),
-                in_=pair[:].rearrange("q (t p) -> q p t", t=PACK),
-            )
-            nc.sync.dma_start(out=out[:, g * K_PASS : (g + 1) * K_PASS], in_=ordered[:])
 
         STEPS = PASSES + LAG + 1
         FIRST_COSINES = PASSES + 3
+        LAST_COSINES = STEPS - 1
         done = 0
 
         with tc.manual_schedule():
@@ -265,13 +270,20 @@ def tile_hopfieldretrievalmodel_pa_k_kernel(tc, xi, memory, out):
                         in_=output_grouped[:],
                     )
                 if step >= FIRST_COSINES:
-                    due = PASSES * (step - FIRST_COSINES + 1) // (STEPS - FIRST_COSINES)
-                    for g in range(done, min(due, u - 1)):
-                        cosines(g)
-                    quantise_rows(u - 1)
-                    for g in range(max(done, u - 1), due):
-                        cosines(g)
+                    pairs = PASSES // 2 - 1
+                    due = (pairs - 2) * (step - FIRST_COSINES + 1) // (LAST_COSINES - FIRST_COSINES)
+                    if step == LAST_COSINES:
+                        due = pairs
+                    for i in range(done, due):
+                        cosines(
+                            2 * i, 2 * i + 2, nc.scalar.copy if i % 2 else nc.vector.tensor_copy
+                        )
                     done = due
+                    if step == LAST_COSINES:
+                        cosines(PASSES - 2, PASSES - 1, nc.scalar.copy)
+                    quantise_rows(u - 1)
+                    if step == LAST_COSINES:
+                        cosines(PASSES - 1, PASSES, nc.vector.tensor_copy)
                 if 0 <= u < PASSES:
                     turn_rows(u)
                 if step == 0:
@@ -286,11 +298,11 @@ def tile_hopfieldretrievalmodel_pa_k_kernel(tc, xi, memory, out):
                 if 1 <= step <= PASSES:
                     retrieve(step - 1)
                 if 0 <= u < PASSES:
-                    group_features(u, 0)
+                    group_features(u, 0, nc.scalar.copy)
                 if step < PASSES:
                     square_row(step, 2)
                 if 0 <= u < PASSES:
-                    group_features(u, 1)
+                    group_features(u, 1, nc.scalar.copy)
                 if step < PASSES:
                     square_row(step, 3)
 

@@ -40,10 +40,9 @@ def tile_hopfieldretrievalmodel_pa_k_kernel(tc, xi, memory, out):
         unit_pool = stack.enter_context(tc.tile_pool(name="unit", bufs=PASSES - LAG + 3))
         norm_pool = stack.enter_context(tc.tile_pool(name="norm", bufs=LAG // GROUP + 3))
         xi_pool = stack.enter_context(tc.tile_pool(name="xi", bufs=3))
-        grouped_pool = stack.enter_context(tc.tile_pool(name="grouped", bufs=4))
+        wide_pool = stack.enter_context(tc.tile_pool(name="wide", bufs=8))
         codes_pool = stack.enter_context(tc.tile_pool(name="codes", bufs=6))
         squares_pool = stack.enter_context(tc.tile_pool(name="squares", bufs=16))
-        store_pool = stack.enter_context(tc.tile_pool(name="store", bufs=4))
         output_pool = stack.enter_context(tc.psum_pool(name="output", bufs=1))
         bank_pool = stack.enter_context(tc.psum_pool(name="bank", bufs=7))
 
@@ -56,6 +55,7 @@ def tile_hopfieldretrievalmodel_pa_k_kernel(tc, xi, memory, out):
         xi_scales_of = {}
         squares_of = {}
         inverse_of = {}
+        pair_of = {}
         unit_turned_of = {}
         unit_codes_of = {}
         unit_scales_of = {}
@@ -75,8 +75,9 @@ def tile_hopfieldretrievalmodel_pa_k_kernel(tc, xi, memory, out):
             nc.sync.dma_start(out=xi_of[group][:], in_=xi[:, first : first + GROUP * K_PASS])
 
         load_rows(0)
+        load_rows(1)
         load_xi(0)
-        for g in range(1, AHEAD):
+        for g in range(2, AHEAD):
             load_rows(g)
         load_xi(1)
 
@@ -101,7 +102,7 @@ def tile_hopfieldretrievalmodel_pa_k_kernel(tc, xi, memory, out):
                     )
             xi_turned_of[group, half] = turned
 
-        def group_xi(group, half, copy):
+        def group_xi(group, half):
             if half == 0:
                 xi_grouped_of[group] = xi_pool.tile(
                     [P, GROUP * QUERIES * PACK], BF16, name="xi_grouped", align_bytes=64
@@ -109,7 +110,7 @@ def tile_hopfieldretrievalmodel_pa_k_kernel(tc, xi, memory, out):
             words = xi_grouped_of[group][:].bitcast(F32).rearrange(
                 "p (g q u) -> p g q u", g=GROUP, u=PAIR
             )
-            copy(
+            nc.vector.tensor_copy(
                 out=words[:, 2 * half : 2 * half + 2],
                 in_=xi_turned_of[group, half][:].rearrange("p g u q -> p g q u"),
             )
@@ -128,7 +129,7 @@ def tile_hopfieldretrievalmodel_pa_k_kernel(tc, xi, memory, out):
             )
 
         def group_patterns(g):
-            grouped_of[g] = grouped_pool.tile([P, FEATURES, PACK], BF16, name="grouped", align_bytes=64)
+            grouped_of[g] = wide_pool.tile([P, FEATURES, PACK], BF16, name="wide", align_bytes=64)
             nc.vector.tensor_copy(
                 out=grouped_of[g][:].rearrange("p (c i) t -> p c t i", i=RUN),
                 in_=rows_of[g][:].rearrange("p t (c i) -> p c t i", i=RUN),
@@ -170,6 +171,16 @@ def tile_hopfieldretrievalmodel_pa_k_kernel(tc, xi, memory, out):
         def clamp(sums):
             nc.vector.tensor_scalar_max(sums, sums, TINY * TINY)
 
+        def invert_norms(group, place):
+            sums = squares_of[group]
+            if place == 0:
+                clamp(sums[:])
+            if place == 1:
+                nc.scalar.sqrt(sums[:], sums[:])
+            if place == 2:
+                inverse_of[group] = norm_pool.tile([P, GROUP * PACK], F32, name="inverse_norm")
+                nc.vector.reciprocal(inverse_of[group][:], sums[:])
+
         def scale_rows(g):
             group, place = divmod(g, GROUP)
             for t in range(PACK):
@@ -193,9 +204,9 @@ def tile_hopfieldretrievalmodel_pa_k_kernel(tc, xi, memory, out):
                         )
                 unit_turned_of[g, half] = turned
 
-        def group_features(g, half, copy):
+        def group_features(g, half):
             words = rows_of[g][:].bitcast(F32).rearrange("c t (p u) -> c t p u", u=PAIR)
-            copy(
+            nc.scalar.copy(
                 out=words[:, 2 * half : 2 * half + 2],
                 in_=unit_turned_of[g, half][:].rearrange("c i u r -> c i r u"),
             )
@@ -217,137 +228,168 @@ def tile_hopfieldretrievalmodel_pa_k_kernel(tc, xi, memory, out):
         output_codes = consts.tile([P, QUERIES], U32, align_bytes=64)
         output_scales = consts.tile([P, QUERIES], U8, align_bytes=64)
 
-        def cosines(first, last, copy):
-            ordered = store_pool.tile([QUERIES, last - first, K_PASS], F32, name="ordered")
-            for g in range(first, last):
-                pair = bank_pool.tile([QUERIES, K_PASS], F32, name="bank")
-                nc.tensor.matmul_mx(
-                    out=pair[:],
-                    lhsT=output_codes[:].bitcast(FP8X4),
-                    lhsT_scale=output_scales[:],
-                    rhs=unit_codes_of[g][:].bitcast(FP8X4),
-                    rhs_scale=unit_scales_of[g][:],
-                    start=True,
-                    stop=True,
+        def square_output():
+            nc.scalar.activation(
+                out=output_squares[:], in_=output[:], func=ACT.Square, accum_out=output_norm[:]
+            )
+
+        def scale_output():
+            nc.scalar.activation(
+                out=output_unit[:], in_=output[:], func=ACT.Copy, scale=output_inverse[:]
+            )
+
+        output_turned = {}
+
+        def turn_output():
+            words = output_unit[:].bitcast(F32)
+            output_turned[0] = bank_pool.tile([P, PAIR, QUERIES], F32, name="bank")
+            for u in range(PAIR):
+                nc.tensor.transpose(
+                    output_turned[0][:, u, :], words[:, u * P : (u + 1) * P], identity[:]
                 )
+
+        def group_output():
+            nc.scalar.copy(
+                out=output_grouped[:].bitcast(F32).rearrange("c (q u) -> c q u", u=PAIR),
+                in_=output_turned[0][:].rearrange("c u q -> c q u"),
+            )
+
+        def quantise_output():
+            nc.vector.quantize_mx(
+                out=output_codes[:].bitcast(FP8X4), scales=output_scales[:], in_=output_grouped[:]
+            )
+
+        def multiply(g):
+            pair_of[g] = bank_pool.tile([QUERIES, K_PASS], F32, name="bank")
+            nc.tensor.matmul_mx(
+                out=pair_of[g][:],
+                lhsT=output_codes[:].bitcast(FP8X4),
+                lhsT_scale=output_scales[:],
+                rhs=unit_codes_of[g][:].bitcast(FP8X4),
+                rhs_scale=unit_scales_of[g][:],
+                start=True,
+                stop=True,
+            )
+
+        def store(first, last, on_scalar):
+            copy = nc.scalar.copy if on_scalar else nc.vector.tensor_copy
+            ordered = wide_pool.tile(
+                [QUERIES, last - first, K_PASS], F32, name="wide", align_bytes=64
+            )
+            for g in range(first, last):
                 copy(
                     out=ordered[:, g - first, :].rearrange("q (p t) -> q p t", t=PACK),
-                    in_=pair[:].rearrange("q (t p) -> q p t", t=PACK),
+                    in_=pair_of[g][:].rearrange("q (t p) -> q p t", t=PACK),
                 )
             nc.sync.dma_start(
                 out=out[:, first * K_PASS : last * K_PASS],
                 in_=ordered[:].rearrange("q g k -> q (g k)"),
             )
 
-        STEPS = PASSES + LAG + 1
-        FIRST_COSINES = PASSES + 3
-        LAST_COSINES = STEPS - 1
-        done = 0
-
         with tc.manual_schedule():
-            for step in range(STEPS):
+            for step in range(PASSES):
                 group, place = divmod(step, GROUP)
                 u = step - LAG
-
                 if step + AHEAD < PASSES:
                     load_rows(step + AHEAD)
                 if place == 0 and group + 2 < GROUPS:
                     load_xi(group + 2)
-
-                if 0 <= u < PASSES:
+                if u >= 0:
                     scale_rows(u)
-                if step == PASSES + 1:
-                    clamp(output_norm[:])
-                    nc.scalar.sqrt(output_norm[:], output_norm[:])
-                if PASSES < step < FIRST_COSINES:
-                    quantise_rows(u - 1)
-                if step == PASSES + 1:
-                    nc.vector.reciprocal(output_inverse[:], output_norm[:])
-                if step == FIRST_COSINES - 1:
-                    nc.vector.quantize_mx(
-                        out=output_codes[:].bitcast(FP8X4),
-                        scales=output_scales[:],
-                        in_=output_grouped[:],
-                    )
-                if step >= FIRST_COSINES:
-                    pairs = PASSES // 2 - 1
-                    due = (pairs - 2) * (step - FIRST_COSINES + 1) // (LAST_COSINES - FIRST_COSINES)
-                    if step == LAST_COSINES:
-                        due = pairs
-                    for i in range(done, due):
-                        cosines(
-                            2 * i, 2 * i + 2, nc.scalar.copy if i % 2 else nc.vector.tensor_copy
-                        )
-                    done = due
-                    if step == LAST_COSINES:
-                        cosines(PASSES - 2, PASSES - 1, nc.scalar.copy)
-                    quantise_rows(u - 1)
-                    if step == LAST_COSINES:
-                        cosines(PASSES - 1, PASSES, nc.vector.tensor_copy)
-                if 0 <= u < PASSES:
                     turn_rows(u)
                 if step == 0:
                     for half in range(2):
                         turn_xi(0, half)
                 if place < 2 and group + 1 < GROUPS:
                     turn_xi(group + 1, place)
-                if step < PASSES:
-                    group_patterns(step)
-                    square_row(step, 0)
-                    square_row(step, 1)
-                if 1 <= step <= PASSES:
-                    retrieve(step - 1)
-                if 0 <= u < PASSES:
-                    group_features(u, 0, nc.scalar.copy)
-                if step < PASSES:
-                    square_row(step, 2)
-                if 0 <= u < PASSES:
-                    group_features(u, 1, nc.scalar.copy)
-                if step < PASSES:
-                    square_row(step, 3)
-
-                if step == PASSES:
-                    nc.scalar.activation(
-                        out=output_squares[:],
-                        in_=output[:],
-                        func=ACT.Square,
-                        accum_out=output_norm[:],
-                    )
-                if step == PASSES + 1:
-                    nc.scalar.activation(
-                        out=output_unit[:], in_=output[:], func=ACT.Copy, scale=output_inverse[:]
-                    )
-                    turned = bank_pool.tile([P, PAIR, QUERIES], F32, name="bank")
-                    words = output_unit[:].bitcast(F32)
-                    for w in range(PAIR):
-                        nc.tensor.transpose(
-                            turned[:, w, :], words[:, w * P : (w + 1) * P], identity[:]
-                        )
-                    nc.scalar.copy(
-                        out=output_grouped[:].bitcast(F32).rearrange("c (q u) -> c q u", u=PAIR),
-                        in_=turned[:].rearrange("c u q -> c q u"),
-                    )
-
-                if step == 0:
+                group_patterns(step)
+                if step == 1:
                     for half in range(2):
-                        group_xi(0, half, nc.vector.tensor_copy)
+                        group_xi(0, half)
                     quantise_xi(0)
+                if step > 0:
+                    retrieve(step - 1)
+                square_row(step, 0)
+                square_row(step, 1)
+                if u >= 0:
+                    group_features(u, 0)
+                square_row(step, 2)
+                if u >= 0:
+                    group_features(u, 1)
+                square_row(step, 3)
                 if group + 1 < GROUPS:
                     if 1 <= place <= 2:
-                        group_xi(group + 1, place - 1, nc.vector.tensor_copy)
+                        group_xi(group + 1, place - 1)
                     if place == 3:
                         quantise_xi(group + 1)
-
-                if 1 <= u and step <= PASSES:
+                if u >= 1:
                     quantise_rows(u - 1)
+                if group > 0:
+                    invert_norms(group - 1, place)
 
-                if 1 <= group <= GROUPS:
-                    sums = squares_of[group - 1]
-                    if place == 0:
-                        clamp(sums[:])
-                    if place == 1:
-                        nc.scalar.sqrt(sums[:], sums[:])
-                    if place == 2:
-                        inverse = norm_pool.tile([P, GROUP * PACK], F32, name="inverse_norm")
-                        nc.vector.reciprocal(inverse[:], sums[:])
-                        inverse_of[group - 1] = inverse
+            first = PASSES - LAG
+            pairs = PASSES // 2 - 2
+            done = 0
+            for u in range(first, PASSES):
+                if u == first:
+                    scale_rows(u)
+                    turn_rows(u)
+                    retrieve(PASSES - 1)
+                    square_output()
+                    group_features(u, 0)
+                    if u + 1 < PASSES:
+                        scale_rows(u + 1)
+                        turn_rows(u + 1)
+                    quantise_rows(u - 1)
+                elif u == first + 1:
+                    clamp(output_norm[:])
+                    nc.scalar.sqrt(output_norm[:], output_norm[:])
+                    group_features(u - 1, 1)
+                    nc.vector.reciprocal(output_inverse[:], output_norm[:])
+                    scale_output()
+                    if u + 1 < PASSES:
+                        scale_rows(u + 1)
+                        turn_rows(u + 1)
+                    quantise_rows(u - 1)
+                    turn_output()
+                    group_features(u, 0)
+                    group_output()
+                    group_features(u, 1)
+                elif u == first + 2:
+                    quantise_output()
+                    due = (pairs - 0) * (u - first - 1) // (LAG - 3)
+                    if u == PASSES - 1:
+                        due = pairs
+                    for g in range(2 * done, 2 * due):
+                        multiply(g)
+                    if u + 1 < PASSES:
+                        scale_rows(u + 1)
+                        turn_rows(u + 1)
+                    quantise_rows(u - 1)
+                    group_features(u, 0)
+                    group_features(u, 1)
+                else:
+                    for i in range(done, due):
+                        store(2 * i, 2 * i + 2, i % 2)
+                    done = due
+                    due = (pairs - 0) * (u - first - 1) // (LAG - 3)
+                    if u == PASSES - 1:
+                        due = pairs
+                    for g in range(2 * done, 2 * due):
+                        multiply(g)
+                    if u + 1 < PASSES:
+                        scale_rows(u + 1)
+                        turn_rows(u + 1)
+                    quantise_rows(u - 1)
+                    group_features(u, 0)
+                    group_features(u, 1)
+                if u < first + GROUP:
+                    invert_norms(GROUPS - 1, u - first)
+            for i in range(done, pairs):
+                store(2 * i, 2 * i + 2, i % 2)
+            for g in range(2 * pairs, PASSES - 1):
+                multiply(g)
+            quantise_rows(PASSES - 1)
+            multiply(PASSES - 1)
+            for g in range(2 * pairs, PASSES):
+                store(g, g + 1, (g + 1) % 2)

@@ -21,6 +21,7 @@ FEATURES = 512
 TINY = 1e-12
 
 PASSES = PATTERNS // K_PASS
+NORM_GROUP = 8
 GROUP = 4
 GROUPS = PASSES // GROUP
 LAG = 14
@@ -110,7 +111,8 @@ def tile_hopfieldretrievalmodel_pa_k_kernel(tc, xi, memory, out):
             words = xi_grouped_of[group][:].bitcast(F32).rearrange(
                 "p (g q u) -> p g q u", g=GROUP, u=PAIR
             )
-            nc.vector.tensor_copy(
+            copy = nc.scalar.copy if half == 1 and group % 2 == 1 else nc.vector.tensor_copy
+            copy(
                 out=words[:, 2 * half : 2 * half + 2],
                 in_=xi_turned_of[group, half][:].rearrange("p g u q -> p g q u"),
             )
@@ -156,9 +158,9 @@ def tile_hopfieldretrievalmodel_pa_k_kernel(tc, xi, memory, out):
             )
 
         def square_row(g, t):
-            group, place = divmod(g, GROUP)
+            group, place = divmod(g, NORM_GROUP)
             if place == 0 and t == 0:
-                squares_of[group] = norm_pool.tile([P, GROUP * PACK], F32, name="sum_of_squares")
+                squares_of[group] = norm_pool.tile([P, NORM_GROUP * PACK], F32, name="sum_of_squares")
             squares = squares_pool.tile([P, FEATURES], BF16, name="squares")
             column = place * PACK + t
             nc.scalar.activation(
@@ -178,11 +180,11 @@ def tile_hopfieldretrievalmodel_pa_k_kernel(tc, xi, memory, out):
             if place == 1:
                 nc.scalar.sqrt(sums[:], sums[:])
             if place == 2:
-                inverse_of[group] = norm_pool.tile([P, GROUP * PACK], F32, name="inverse_norm")
+                inverse_of[group] = norm_pool.tile([P, NORM_GROUP * PACK], F32, name="inverse_norm")
                 nc.vector.reciprocal(inverse_of[group][:], sums[:])
 
         def scale_rows(g):
-            group, place = divmod(g, GROUP)
+            group, place = divmod(g, NORM_GROUP)
             for t in range(PACK):
                 column = place * PACK + t
                 nc.vector.tensor_scalar_mul(
@@ -324,8 +326,8 @@ def tile_hopfieldretrievalmodel_pa_k_kernel(tc, xi, memory, out):
                         quantise_xi(group + 1)
                 if u >= 1:
                     quantise_rows(u - 1)
-                if group > 0:
-                    invert_norms(group - 1, place)
+                if step >= NORM_GROUP:
+                    invert_norms(step // NORM_GROUP - 1, step % NORM_GROUP)
 
             first = PASSES - LAG
             pairs = PASSES // 2 - 2
@@ -370,7 +372,7 @@ def tile_hopfieldretrievalmodel_pa_k_kernel(tc, xi, memory, out):
                     group_features(u, 1)
                 else:
                     for i in range(done, due):
-                        store(2 * i, 2 * i + 2, i % 2)
+                        store(2 * i, 2 * i + 2, i % 2 or i % 8 == 0)
                     done = due
                     due = (pairs - 0) * (u - first - 1) // (LAG - 3)
                     if u == PASSES - 1:
@@ -383,8 +385,7 @@ def tile_hopfieldretrievalmodel_pa_k_kernel(tc, xi, memory, out):
                     quantise_rows(u - 1)
                     group_features(u, 0)
                     group_features(u, 1)
-                if u < first + GROUP:
-                    invert_norms(GROUPS - 1, u - first)
+                invert_norms(PASSES // NORM_GROUP - 1, u - first)
             for i in range(done, pairs):
                 store(2 * i, 2 * i + 2, i % 2)
             for g in range(2 * pairs, PASSES - 1):

@@ -111,8 +111,7 @@ def tile_hopfieldretrievalmodel_pa_k_kernel(tc, xi, memory, out):
             words = xi_grouped_of[group][:].bitcast(F32).rearrange(
                 "p (g q u) -> p g q u", g=GROUP, u=PAIR
             )
-            copy = nc.scalar.copy if half == 1 and group % 2 == 1 else nc.vector.tensor_copy
-            copy(
+            nc.vector.tensor_copy(
                 out=words[:, 2 * half : 2 * half + 2],
                 in_=xi_turned_of[group, half][:].rearrange("p g u q -> p g q u"),
             )
@@ -261,6 +260,12 @@ def tile_hopfieldretrievalmodel_pa_k_kernel(tc, xi, memory, out):
                 out=output_codes[:].bitcast(FP8X4), scales=output_scales[:], in_=output_grouped[:]
             )
 
+        def warm_tensor(count):
+            rows = rows_of[PASSES - 1][:, 0, :]
+            for i in range(count):
+                unused = bank_pool.tile([P, FEATURES], F32, name="bank")
+                nc.tensor.matmul(out=unused[:], lhsT=rows[:, :P], rhs=rows, start=True, stop=True)
+
         def multiply(g):
             pair_of[g] = bank_pool.tile([QUERIES, K_PASS], F32, name="bank")
             nc.tensor.matmul_mx(
@@ -342,6 +347,7 @@ def tile_hopfieldretrievalmodel_pa_k_kernel(tc, xi, memory, out):
                     if u + 1 < PASSES:
                         scale_rows(u + 1)
                         turn_rows(u + 1)
+                    warm_tensor(3)
                     quantise_rows(u - 1)
                 elif u == first + 1:
                     clamp(output_norm[:])
@@ -354,6 +360,7 @@ def tile_hopfieldretrievalmodel_pa_k_kernel(tc, xi, memory, out):
                         turn_rows(u + 1)
                     quantise_rows(u - 1)
                     turn_output()
+                    warm_tensor(3)
                     group_features(u, 0)
                     group_output()
                     group_features(u, 1)

@@ -24,7 +24,7 @@ PASSES = PATTERNS // K_PASS
 NORM_GROUP = 8
 GROUP = 4
 GROUPS = PASSES // GROUP
-LAG = 14
+LAG = 16
 RUN = 8
 AHEAD = 3
 
@@ -41,9 +41,10 @@ def tile_hopfieldretrievalmodel_pa_k_kernel(tc, xi, memory, out):
         unit_pool = stack.enter_context(tc.tile_pool(name="unit", bufs=PASSES - LAG + 3))
         norm_pool = stack.enter_context(tc.tile_pool(name="norm", bufs=LAG // GROUP + 3))
         xi_pool = stack.enter_context(tc.tile_pool(name="xi", bufs=3))
+        xi_codes_pool = stack.enter_context(tc.tile_pool(name="xi_codes", bufs=2))
         wide_pool = stack.enter_context(tc.tile_pool(name="wide", bufs=8))
         codes_pool = stack.enter_context(tc.tile_pool(name="codes", bufs=6))
-        squares_pool = stack.enter_context(tc.tile_pool(name="squares", bufs=16))
+        squares_pool = stack.enter_context(tc.tile_pool(name="squares", bufs=24))
         output_pool = stack.enter_context(tc.psum_pool(name="output", bufs=1))
         bank_pool = stack.enter_context(tc.psum_pool(name="bank", bufs=7))
 
@@ -105,7 +106,7 @@ def tile_hopfieldretrievalmodel_pa_k_kernel(tc, xi, memory, out):
 
         def group_xi(group, half):
             if half == 0:
-                xi_grouped_of[group] = xi_pool.tile(
+                xi_grouped_of[group] = xi_codes_pool.tile(
                     [P, GROUP * QUERIES * PACK], BF16, name="xi_grouped", align_bytes=64
                 )
             words = xi_grouped_of[group][:].bitcast(F32).rearrange(
@@ -117,10 +118,10 @@ def tile_hopfieldretrievalmodel_pa_k_kernel(tc, xi, memory, out):
             )
 
         def quantise_xi(group):
-            xi_codes_of[group] = xi_pool.tile(
+            xi_codes_of[group] = xi_codes_pool.tile(
                 [P, GROUP * QUERIES], U32, name="xi_codes", align_bytes=64
             )
-            xi_scales_of[group] = xi_pool.tile(
+            xi_scales_of[group] = xi_codes_pool.tile(
                 [P, GROUP * QUERIES], U8, name="xi_scales", align_bytes=64
             )
             nc.vector.quantize_mx(
@@ -215,11 +216,16 @@ def tile_hopfieldretrievalmodel_pa_k_kernel(tc, xi, memory, out):
         def quantise_rows(g):
             unit_codes_of[g] = unit_pool.tile([P, K_PASS], U32, name="unit_codes", align_bytes=64)
             unit_scales_of[g] = unit_pool.tile([P, K_PASS], U8, name="unit_scales", align_bytes=64)
-            nc.vector.quantize_mx(
-                out=unit_codes_of[g][:].bitcast(FP8X4),
-                scales=unit_scales_of[g][:],
-                in_=rows_of[g][:].rearrange("c t d -> c (t d)"),
-            )
+            parts = 2 if g == PASSES - 1 else 1
+            columns = K_PASS // parts
+            rows = PACK // parts
+            for i in range(parts):
+                part = slice(i * columns, (i + 1) * columns)
+                nc.vector.quantize_mx(
+                    out=unit_codes_of[g][:, part].bitcast(FP8X4),
+                    scales=unit_scales_of[g][:, part],
+                    in_=rows_of[g][:, i * rows : (i + 1) * rows, :].rearrange("c t d -> c (t d)"),
+                )
 
         output_squares = consts.tile([QUERIES, FEATURES], BF16)
         output_norm = consts.tile([QUERIES, 1], F32)
@@ -268,15 +274,19 @@ def tile_hopfieldretrievalmodel_pa_k_kernel(tc, xi, memory, out):
 
         def multiply(g):
             pair_of[g] = bank_pool.tile([QUERIES, K_PASS], F32, name="bank")
-            nc.tensor.matmul_mx(
-                out=pair_of[g][:],
-                lhsT=output_codes[:].bitcast(FP8X4),
-                lhsT_scale=output_scales[:],
-                rhs=unit_codes_of[g][:].bitcast(FP8X4),
-                rhs_scale=unit_scales_of[g][:],
-                start=True,
-                stop=True,
-            )
+            parts = 2 if g == PASSES - 1 else 1
+            columns = K_PASS // parts
+            for i in range(parts):
+                part = slice(i * columns, (i + 1) * columns)
+                nc.tensor.matmul_mx(
+                    out=pair_of[g][:, part],
+                    lhsT=output_codes[:].bitcast(FP8X4),
+                    lhsT_scale=output_scales[:],
+                    rhs=unit_codes_of[g][:, part].bitcast(FP8X4),
+                    rhs_scale=unit_scales_of[g][:, part],
+                    start=True,
+                    stop=True,
+                )
 
         def store(first, last, on_scalar):
             copy = nc.scalar.copy if on_scalar else nc.vector.tensor_copy

@@ -24,7 +24,7 @@ PASSES = PATTERNS // K_PASS
 NORM_GROUP = 8
 GROUP = 4
 GROUPS = PASSES // GROUP
-LAG = 16
+LAG = 18
 RUN = 8
 AHEAD = 3
 
@@ -42,7 +42,7 @@ def tile_hopfieldretrievalmodel_pa_k_kernel(tc, xi, memory, out):
         norm_pool = stack.enter_context(tc.tile_pool(name="norm", bufs=LAG // GROUP + 3))
         xi_pool = stack.enter_context(tc.tile_pool(name="xi", bufs=3))
         xi_codes_pool = stack.enter_context(tc.tile_pool(name="xi_codes", bufs=2))
-        wide_pool = stack.enter_context(tc.tile_pool(name="wide", bufs=8))
+        wide_pool = stack.enter_context(tc.tile_pool(name="wide", bufs=6))
         codes_pool = stack.enter_context(tc.tile_pool(name="codes", bufs=6))
         squares_pool = stack.enter_context(tc.tile_pool(name="squares", bufs=24))
         output_pool = stack.enter_context(tc.psum_pool(name="output", bufs=1))
@@ -293,15 +293,22 @@ def tile_hopfieldretrievalmodel_pa_k_kernel(tc, xi, memory, out):
             ordered = wide_pool.tile(
                 [QUERIES, last - first, K_PASS], F32, name="wide", align_bytes=64
             )
-            for g in range(first, last):
-                copy(
-                    out=ordered[:, g - first, :].rearrange("q (p t) -> q p t", t=PACK),
-                    in_=pair_of[g][:].rearrange("q (t p) -> q p t", t=PACK),
+            parts = 2 if first == PASSES - 1 else 1
+            size = P // parts
+            for i in range(parts):
+                part = slice(i * size, (i + 1) * size)
+                columns = slice(i * size * PACK, (i + 1) * size * PACK)
+                for g in range(first, last):
+                    copy(
+                        out=ordered[:, g - first, columns].rearrange("q (p t) -> q p t", t=PACK),
+                        in_=pair_of[g][:].rearrange("q (t p) -> q p t", t=PACK)[:, part, :],
+                    )
+                nc.sync.dma_start(
+                    out=out[:, first * K_PASS : last * K_PASS].rearrange(
+                        "q (g k) -> q g k", k=K_PASS
+                    )[:, :, columns],
+                    in_=ordered[:, :, columns],
                 )
-            nc.sync.dma_start(
-                out=out[:, first * K_PASS : last * K_PASS],
-                in_=ordered[:].rearrange("q g k -> q (g k)"),
-            )
 
         with tc.manual_schedule():
             for step in range(PASSES):
@@ -407,7 +414,9 @@ def tile_hopfieldretrievalmodel_pa_k_kernel(tc, xi, memory, out):
                 store(2 * i, 2 * i + 2, i % 2)
             for g in range(2 * pairs, PASSES - 1):
                 multiply(g)
+            store(PASSES - 4, PASSES - 3, 0)
+            store(PASSES - 3, PASSES - 2, 1)
             quantise_rows(PASSES - 1)
             multiply(PASSES - 1)
-            for g in range(2 * pairs, PASSES):
-                store(g, g + 1, (g + 1) % 2)
+            store(PASSES - 2, PASSES - 1, 1)
+            store(PASSES - 1, PASSES, 0)

from contextlib import ExitStack

import concourse.mybir as mybir
from concourse.masks import make_identity

F32 = mybir.dt.float32
BF16 = mybir.dt.bfloat16
U32 = mybir.dt.uint32
U8 = mybir.dt.uint8
FP8X4 = mybir.dt.float8_e4m3fn_x4
ACT = mybir.ActivationFunctionType

P = 128
PACK = 4
K_PASS = P * PACK
PAIR = 2

QUERIES = 128
PATTERNS = 16384
FEATURES = 512
TINY = 1e-12

PASSES = PATTERNS // K_PASS
NORM_GROUP = 8
GROUP = 4
GROUPS = PASSES // GROUP
LAG = 18
RUN = 8
AHEAD = 3

FLOPS = 2 * 2 * QUERIES * PATTERNS * FEATURES

assert QUERIES == P and FEATURES == K_PASS and GROUPS * GROUP == PASSES


def tile_hopfieldretrievalmodel_pa_k_kernel(tc, xi, memory, out):
    nc = tc.nc
    with ExitStack() as stack:
        consts = stack.enter_context(tc.tile_pool(name="consts", bufs=1))
        rows_pool = stack.enter_context(tc.tile_pool(name="rows", bufs=LAG + AHEAD + 3))
        unit_pool = stack.enter_context(tc.tile_pool(name="unit", bufs=PASSES - LAG + 3))
        norm_pool = stack.enter_context(tc.tile_pool(name="norm", bufs=LAG // GROUP + 3))
        xi_pool = stack.enter_context(tc.tile_pool(name="xi", bufs=3))
        xi_codes_pool = stack.enter_context(tc.tile_pool(name="xi_codes", bufs=2))
        wide_pool = stack.enter_context(tc.tile_pool(name="wide", bufs=6))
        codes_pool = stack.enter_context(tc.tile_pool(name="codes", bufs=6))
        squares_pool = stack.enter_context(tc.tile_pool(name="squares", bufs=24))
        output_pool = stack.enter_context(tc.psum_pool(name="output", bufs=1))
        bank_pool = stack.enter_context(tc.psum_pool(name="bank", bufs=7))

        rows_of = {}
        grouped_of = {}
        xi_of = {}
        xi_turned_of = {}
        xi_grouped_of = {}
        xi_codes_of = {}
        xi_scales_of = {}
        squares_of = {}
        inverse_of = {}
        pair_of = {}
        unit_turned_of = {}
        unit_codes_of = {}
        unit_scales_of = {}

        def load_rows(g):
            rows_of[g] = rows_pool.tile([P, PACK, FEATURES], BF16, name="rows", align_bytes=64)
            source = memory[g * K_PASS : (g + 1) * K_PASS, :].rearrange("(p t) d -> p t d", t=PACK)
            pieces = PACK if g == 0 else 1
            size = PACK // pieces
            for i in range(pieces):
                piece = slice(i * size, (i + 1) * size)
                nc.sync.dma_start(out=rows_of[g][:, piece, :], in_=source[:, piece, :])

        def load_xi(group):
            first = group * GROUP * K_PASS
            xi_of[group] = xi_pool.tile([QUERIES, GROUP * K_PASS], BF16, name="xi_columns")
            nc.sync.dma_start(out=xi_of[group][:], in_=xi[:, first : first + GROUP * K_PASS])

        load_rows(0)
        load_rows(1)
        load_xi(0)
        for g in range(2, AHEAD):
            load_rows(g)
        load_xi(1)

        identity = consts.tile([P, P], F32)
        make_identity(nc, identity[:])
        one = consts.tile([P, 1], F32)
        nc.vector.memset(one[:], 1.0)
        warm = consts.tile([P, 1], F32)
        nc.scalar.sqrt(warm[:], one[:])

        output = output_pool.tile([QUERIES, FEATURES], F32)

        def turn_xi(group, half):
            words = xi_of[group][:].bitcast(F32).rearrange(
                "q (g p u) -> q g u p", g=GROUP, u=PAIR
            )
            turned = bank_pool.tile([P, 2, PAIR, QUERIES], F32, name="bank")
            for i in range(2):
                for u in range(PAIR):
                    nc.tensor.transpose(
                        turned[:, i, u, :], words[:, 2 * half + i, u, :], identity[:]
                    )
            xi_turned_of[group, half] = turned

        def group_xi(group, half):
            if half == 0:
                xi_grouped_of[group] = xi_codes_pool.tile(
                    [P, GROUP * QUERIES * PACK], BF16, name="xi_grouped", align_bytes=64
                )
            words = xi_grouped_of[group][:].bitcast(F32).rearrange(
                "p (g q u) -> p g q u", g=GROUP, u=PAIR
            )
            nc.vector.tensor_copy(
                out=words[:, 2 * half : 2 * half + 2],
                in_=xi_turned_of[group, half][:].rearrange("p g u q -> p g q u"),
            )

        def quantise_xi(group):
            xi_codes_of[group] = xi_codes_pool.tile(
                [P, GROUP * QUERIES], U32, name="xi_codes", align_bytes=64
            )
            xi_scales_of[group] = xi_codes_pool.tile(
                [P, GROUP * QUERIES], U8, name="xi_scales", align_bytes=64
            )
            nc.vector.quantize_mx(
                out=xi_codes_of[group][:].bitcast(FP8X4),
                scales=xi_scales_of[group][:],
                in_=xi_grouped_of[group][:],
            )

        def group_patterns(g):
            grouped_of[g] = wide_pool.tile([P, FEATURES, PACK], BF16, name="wide", align_bytes=64)
            nc.vector.tensor_copy(
                out=grouped_of[g][:].rearrange("p (c i) t -> p c t i", i=RUN),
                in_=rows_of[g][:].rearrange("p t (c i) -> p c t i", i=RUN),
            )

        def retrieve(g):
            codes = codes_pool.tile([P, FEATURES], U32, name="codes", align_bytes=64)
            scales = codes_pool.tile([P, FEATURES], U8, name="scales", align_bytes=64)
            nc.vector.quantize_mx(
                out=codes[:].bitcast(FP8X4),
                scales=scales[:],
                in_=grouped_of[g][:].rearrange("p d t -> p (d t)"),
            )
            group, place = divmod(g, GROUP)
            queries = slice(place * QUERIES, (place + 1) * QUERIES)
            nc.tensor.matmul_mx(
                out=output[:],
                lhsT=xi_codes_of[group][:, queries].bitcast(FP8X4),
                lhsT_scale=xi_scales_of[group][:, queries],
                rhs=codes[:].bitcast(FP8X4),
                rhs_scale=scales[:],
                start=(g == 0),
                stop=(g == PASSES - 1),
            )

        def square_row(g, t):
            group, place = divmod(g, NORM_GROUP)
            if place == 0 and t == 0:
                squares_of[group] = norm_pool.tile([P, NORM_GROUP * PACK], F32, name="sum_of_squares")
            squares = squares_pool.tile([P, FEATURES], BF16, name="squares")
            column = place * PACK + t
            nc.scalar.activation(
                out=squares[:],
                in_=rows_of[g][:, t, :],
                func=ACT.Square,
                accum_out=squares_of[group][:, column : column + 1],
            )

        def clamp(sums):
            nc.vector.tensor_scalar_max(sums, sums, TINY * TINY)

        def invert_norms(group, place):
            sums = squares_of[group]
            if place == 0:
                clamp(sums[:])
            if place == 1:
                nc.scalar.sqrt(sums[:], sums[:])
            if place == 2:
                inverse_of[group] = norm_pool.tile([P, NORM_GROUP * PACK], F32, name="inverse_norm")
                nc.vector.reciprocal(inverse_of[group][:], sums[:])

        def scale_rows(g):
            group, place = divmod(g, NORM_GROUP)
            for t in range(PACK):
                column = place * PACK + t
                nc.vector.tensor_scalar_mul(
                    out=rows_of[g][:, t, :],
                    in0=rows_of[g][:, t, :],
                    scalar1=inverse_of[group][:, column : column + 1],
                )

        def turn_rows(g):
            words = rows_of[g][:].bitcast(F32)
            for half in range(2):
                turned = bank_pool.tile([P, 2, PAIR, P], F32, name="bank")
                for i in range(2):
                    for u in range(PAIR):
                        nc.tensor.transpose(
                            turned[:, i, u, :],
                            words[:, 2 * half + i, u * P : (u + 1) * P],
                            identity[:],
                        )
                unit_turned_of[g, half] = turned

        def group_features(g, half):
            words = rows_of[g][:].bitcast(F32).rearrange("c t (p u) -> c t p u", u=PAIR)
            nc.scalar.copy(
                out=words[:, 2 * half : 2 * half + 2],
                in_=unit_turned_of[g, half][:].rearrange("c i u r -> c i r u"),
            )

        def quantise_rows(g):
            unit_codes_of[g] = unit_pool.tile([P, K_PASS], U32, name="unit_codes", align_bytes=64)
            unit_scales_of[g] = unit_pool.tile([P, K_PASS], U8, name="unit_scales", align_bytes=64)
            parts = 2 if g == PASSES - 1 else 1
            columns = K_PASS // parts
            rows = PACK // parts
            for i in range(parts):
                part = slice(i * columns, (i + 1) * columns)
                nc.vector.quantize_mx(
                    out=unit_codes_of[g][:, part].bitcast(FP8X4),
                    scales=unit_scales_of[g][:, part],
                    in_=rows_of[g][:, i * rows : (i + 1) * rows, :].rearrange("c t d -> c (t d)"),
                )

        output_squares = consts.tile([QUERIES, FEATURES], BF16)
        output_norm = consts.tile([QUERIES, 1], F32)
        output_inverse = consts.tile([QUERIES, 1], F32)
        output_unit = consts.tile([QUERIES, FEATURES], BF16)
        output_grouped = consts.tile([P, QUERIES * PACK], BF16, align_bytes=64)
        output_codes = consts.tile([P, QUERIES], U32, align_bytes=64)
        output_scales = consts.tile([P, QUERIES], U8, align_bytes=64)

        def square_output():
            nc.scalar.activation(
                out=output_squares[:], in_=output[:], func=ACT.Square, accum_out=output_norm[:]
            )

        def scale_output():
            nc.scalar.activation(
                out=output_unit[:], in_=output[:], func=ACT.Copy, scale=output_inverse[:]
            )

        output_turned = {}

        def turn_output():
            words = output_unit[:].bitcast(F32)
            output_turned[0] = bank_pool.tile([P, PAIR, QUERIES], F32, name="bank")
            for u in range(PAIR):
                nc.tensor.transpose(
                    output_turned[0][:, u, :], words[:, u * P : (u + 1) * P], identity[:]
                )

        def group_output():
            nc.scalar.copy(
                out=output_grouped[:].bitcast(F32).rearrange("c (q u) -> c q u", u=PAIR),
                in_=output_turned[0][:].rearrange("c u q -> c q u"),
            )

        def quantise_output():
            nc.vector.quantize_mx(
                out=output_codes[:].bitcast(FP8X4), scales=output_scales[:], in_=output_grouped[:]
            )

        def warm_tensor(count):
            rows = rows_of[PASSES - 1][:, 0, :]
            for i in range(count):
                unused = bank_pool.tile([P, FEATURES], F32, name="bank")
                nc.tensor.matmul(out=unused[:], lhsT=rows[:, :P], rhs=rows, start=True, stop=True)

        def multiply(g):
            pair_of[g] = bank_pool.tile([QUERIES, K_PASS], F32, name="bank")
            parts = 2 if g == PASSES - 1 else 1
            columns = K_PASS // parts
            for i in range(parts):
                part = slice(i * columns, (i + 1) * columns)
                nc.tensor.matmul_mx(
                    out=pair_of[g][:, part],
                    lhsT=output_codes[:].bitcast(FP8X4),
                    lhsT_scale=output_scales[:],
                    rhs=unit_codes_of[g][:, part].bitcast(FP8X4),
                    rhs_scale=unit_scales_of[g][:, part],
                    start=True,
                    stop=True,
                )

        def store(first, last, on_scalar):
            copy = nc.scalar.copy if on_scalar else nc.vector.tensor_copy
            ordered = wide_pool.tile(
                [QUERIES, last - first, K_PASS], F32, name="wide", align_bytes=64
            )
            parts = 2 if first == PASSES - 1 else 1
            size = P // parts
            for i in range(parts):
                part = slice(i * size, (i + 1) * size)
                columns = slice(i * size * PACK, (i + 1) * size * PACK)
                for g in range(first, last):
                    copy(
                        out=ordered[:, g - first, columns].rearrange("q (p t) -> q p t", t=PACK),
                        in_=pair_of[g][:].rearrange("q (t p) -> q p t", t=PACK)[:, part, :],
                    )
                nc.sync.dma_start(
                    out=out[:, first * K_PASS : last * K_PASS].rearrange(
                        "q (g k) -> q g k", k=K_PASS
                    )[:, :, columns],
                    in_=ordered[:, :, columns],
                )

        with tc.manual_schedule():
            for step in range(PASSES):
                group, place = divmod(step, GROUP)
                u = step - LAG
                if step + AHEAD < PASSES:
                    load_rows(step + AHEAD)
                if place == 0 and group + 2 < GROUPS:
                    load_xi(group + 2)
                if u >= 0:
                    scale_rows(u)
                    turn_rows(u)
                if step == 0:
                    for half in range(2):
                        turn_xi(0, half)
                if place < 2 and group + 1 < GROUPS:
                    turn_xi(group + 1, place)
                group_patterns(step)
                if step == 1:
                    for half in range(2):
                        group_xi(0, half)
                    quantise_xi(0)
                if step > 0:
                    retrieve(step - 1)
                square_row(step, 0)
                square_row(step, 1)
                if u >= 0:
                    group_features(u, 0)
                square_row(step, 2)
                if u >= 0:
                    group_features(u, 1)
                square_row(step, 3)
                if group + 1 < GROUPS:
                    if 1 <= place <= 2:
                        group_xi(group + 1, place - 1)
                    if place == 3:
                        quantise_xi(group + 1)
                if u >= 1:
                    quantise_rows(u - 1)
                if step >= NORM_GROUP:
                    invert_norms(step // NORM_GROUP - 1, step % NORM_GROUP)

            first = PASSES - LAG
            pairs = PASSES // 2 - 2
            done = 0
            for u in range(first, PASSES):
                if u == first:
                    scale_rows(u)
                    turn_rows(u)
                    retrieve(PASSES - 1)
                    square_output()
                    group_features(u, 0)
                    if u + 1 < PASSES:
                        scale_rows(u + 1)
                        turn_rows(u + 1)
                    warm_tensor(3)
                    quantise_rows(u - 1)
                elif u == first + 1:
                    clamp(output_norm[:])
                    nc.scalar.sqrt(output_norm[:], output_norm[:])
                    group_features(u - 1, 1)
                    nc.vector.reciprocal(output_inverse[:], output_norm[:])
                    scale_output()
                    if u + 1 < PASSES:
                        scale_rows(u + 1)
                        turn_rows(u + 1)
                    quantise_rows(u - 1)
                    turn_output()
                    warm_tensor(3)
                    group_features(u, 0)
                    group_output()
                    group_features(u, 1)
                elif u == first + 2:
                    quantise_output()
                    due = (pairs - 0) * (u - first - 1) // (LAG - 3)
                    if u == PASSES - 1:
                        due = pairs
                    for g in range(2 * done, 2 * due):
                        multiply(g)
                    if u + 1 < PASSES:
                        scale_rows(u + 1)
                        turn_rows(u + 1)
                    quantise_rows(u - 1)
                    group_features(u, 0)
                    group_features(u, 1)
                else:
                    for i in range(done, due):
                        store(2 * i, 2 * i + 2, i % 2 or i % 8 == 0)
                    done = due
                    due = (pairs - 0) * (u - first - 1) // (LAG - 3)
                    if u == PASSES - 1:
                        due = pairs
                    for g in range(2 * done, 2 * due):
                        multiply(g)
                    if u + 1 < PASSES:
                        scale_rows(u + 1)
                        turn_rows(u + 1)
                    quantise_rows(u - 1)
                    group_features(u, 0)
                    group_features(u, 1)
                invert_norms(PASSES // NORM_GROUP - 1, u - first)
            for i in range(done, pairs):
                store(2 * i, 2 * i + 2, i % 2)
            for g in range(2 * pairs, PASSES - 1):
                multiply(g)
            store(PASSES - 4, PASSES - 3, 0)
            store(PASSES - 3, PASSES - 2, 1)
            quantise_rows(PASSES - 1)
            multiply(PASSES - 1)
            store(PASSES - 2, PASSES - 1, 1)
            store(PASSES - 1, PASSES, 0)
